import numpy as np
import ml_dtypes


def mxq(x, axis, fmt="e4m3"):
    dtype, down = {"e4m3": (ml_dtypes.float8_e4m3fn, 7), "e5m2": (ml_dtypes.float8_e5m2, 14)}[fmt]
    v = np.moveaxis(np.asarray(x, np.float32).astype(ml_dtypes.bfloat16).astype(np.float64), axis, -1)
    blocks = v.reshape(v.shape[:-1] + (-1, 32))
    amax = np.abs(blocks).max(-1, keepdims=True)
    byte = np.maximum(np.where(amax > 0, np.frexp(amax)[1] - 1 + 127, 0) - down, 1)
    scale = np.exp2(byte - 127.0)
    codes = (blocks / scale).astype(np.float32).astype(dtype).astype(np.float64)
    return np.moveaxis((codes * scale).reshape(v.shape), -1, axis)


WIDE = False


def mx_kscale(k):
    if not WIDE:
        return np.ones(k)
    levels = np.array([10, -10, 5, -5, 0])
    if k % 512:
        return np.exp2(np.random.permutation(np.resize(levels, k // 32))).repeat(32)
    a = np.empty((k // 512, 16))
    for p in range(k // 512):
        a[p, :8] = np.random.permutation(np.resize(levels, 8))
        for g in range(8):
            far = levels[np.abs(levels - a[p, g]) >= 10]
            a[p, g + 8] = far[np.random.randint(len(far))]
    return np.exp2(a.ravel()).repeat(32)


BF16 = ml_dtypes.bfloat16


def bf(x):
    return np.asarray(x, np.float32).astype(BF16)


def f64(x):
    return np.asarray(x).astype(np.float64)


B, N, CIN, COUT, CB = 8, 512, 1024, 512, 1024
BN_EPS = 1e-5


def batchnorm(x, gamma, beta):
    mu = x.mean(axis=(0, 1))
    var = x.var(axis=(0, 1))
    return gamma * (x - mu) * (1.0 / np.sqrt(var + BN_EPS)) + beta


def setup_inputs():
    s, t = mx_kscale(CIN), mx_kscale(CB)
    return {"feat": bf(np.random.standard_normal((B, N, CIN)) * s),
            "ag": bf(0.4 + 0.12 * np.random.standard_normal((B, N, CB))),
            "W_feat": bf(np.random.standard_normal((CIN, COUT)) / np.sqrt(CIN) / s[:, None]),
            "b_feat": bf(0.3 * np.random.standard_normal(COUT)),
            "g1": bf((1.0 + 0.1 * np.random.standard_normal(CB)) * t),
            "be1": bf(0.1 * np.random.standard_normal(CB) * t),
            "W_ag": bf(np.random.standard_normal((CB, COUT)) / np.sqrt(CB) / t[:, None]),
            "b_ag": bf(0.3 * np.random.standard_normal(COUT))}


def reference(feat, ag, W_feat, b_feat, g1, be1, W_ag, b_ag):
    self_feat = (mxq(f64(feat), 2, "e4m3") @ mxq(f64(W_feat), 0, "e4m3")) + f64(b_feat)
    h = np.maximum(batchnorm(f64(ag), f64(g1), f64(be1)), 0.0)
    ag_proj = (mxq(h, 2, "e4m3") @ mxq(f64(W_ag), 0, "e4m3")) + f64(b_ag)
    return self_feat + ag_proj

@@ -1,0 +1,319 @@
+from contextlib import ExitStack
+
+import concourse.mybir as mybir
+from concourse.masks import make_identity
+
+BF16 = mybir.dt.bfloat16
+F32 = mybir.dt.float32
+U32 = mybir.dt.uint32
+U8 = mybir.dt.uint8
+FP8X4 = mybir.dt.float8_e4m3fn_x4
+ALU = mybir.AluOpType
+ACT = mybir.ActivationFunctionType
+AXIS = mybir.AxisListType
+
+P = 128
+PACK = 4
+K_PASS = P * PACK
+
+POINTS = 8 * 512
+CHANNELS = 1024
+COUT = 512
+BN_EPS = 1e-5
+
+SUB = 4
+CHUNK = P * SUB
+N_CHUNKS = POINTS // CHUNK
+PASSES = CHANNELS // K_PASS
+CH_TILES = CHANNELS // P
+BN_STATS_DIM = 6
+PSUM_BANKS = 8
+NATURAL_BUFS = 5
+PE_STAT_TILES = 3
+DVE_STAT_TILES = CH_TILES - PE_STAT_TILES
+FEAT_EARLY = 2
+FEAT_AHEAD = 3
+VECTOR_REGROUPS_EVERY = 4
+RUN = 4
+
+FLOPS = 2 * POINTS * (CHANNELS + CHANNELS) * COUT
+
+
+def by_runs_src(rows):
+    return rows.rearrange("p t (c i) -> p c t i", i=RUN)
+
+
+def by_runs_dst(grouped):
+    return grouped.rearrange("p (c i) t -> p c t i", i=RUN)
+
+
+def tile_geoconv_pb_t_kernel(tc, feat, ag, W_feat, b_feat, g1, be1, W_ag, b_ag, out):
+    nc = tc.nc
+    feat_chunks = feat.flatten_outer_dims().rearrange("(c p i) k -> c p i k", p=P, i=SUB)
+    ag_chunks = ag.flatten_outer_dims().rearrange("(c p i) k -> c p i k", p=P, i=SUB)
+    out_chunks = out.flatten_outer_dims().rearrange("(c p i) n -> c p i n", p=P, i=SUB)
+
+    with ExitStack() as ctx:
+        ctx.enter_context(tc.manual_schedule())
+        keep = ctx.enter_context(tc.tile_pool(name="keep", bufs=1))
+
+        ident_bf16 = keep.tile([P, P], BF16)
+        make_identity(nc, ident_bf16[:])
+        ident_f32 = keep.tile([P, P], F32)
+        make_identity(nc, ident_f32[:])
+
+        eps = keep.tile([P, 1], F32)
+        nc.vector.memset(eps[:], BN_EPS)
+        table_warmer = keep.tile([P, 1], F32)
+        nc.scalar.activation(out=table_warmer[:], in_=eps[:], func=ACT.Sqrt)
+
+        ones = keep.tile([P, P], BF16)
+        nc.vector.memset(ones[:], 1.0)
+        vector_rows = keep.tile([P, K_PASS], BF16)
+        nc.vector.memset(vector_rows[:], 0.0)
+        nc.scalar.dma_start(out=vector_rows[0:PASSES, :], in_=g1.rearrange("(g k) -> g k", g=PASSES))
+        nc.scalar.dma_start(out=vector_rows[PASSES : 2 * PASSES, :], in_=be1.rearrange("(g k) -> g k", g=PASSES))
+        bias_rows = keep.tile([P, COUT], BF16)
+        nc.vector.memset(bias_rows[:], 0.0)
+        nc.scalar.dma_start(out=bias_rows[0:1, :], in_=b_feat.rearrange("(o n) -> o n", o=1))
+        nc.scalar.dma_start(out=bias_rows[1:2, :], in_=b_ag.rearrange("(o n) -> o n", o=1))
+        gain_shift = keep.tile([P, 2 * CH_TILES], F32)
+        gain = gain_shift[:, 0:CH_TILES]
+        shift = gain_shift[:, CH_TILES : 2 * CH_TILES]
+        bias = keep.tile([P, COUT], F32)
+
+        ag_t = keep.tile([P, CH_TILES, POINTS], BF16)
+        feat_grouped = keep.tile([P, N_CHUNKS, PASSES, CHUNK * PACK], BF16, align_bytes=64)
+        feat_grouped_words = feat_grouped[:].bitcast(F32)
+        w_codes = keep.tile([P, 2, PASSES, COUT], U32, align_bytes=64)
+        w_scales = keep.tile([P, 2, PASSES, COUT], U8, align_bytes=64)
+        stats = keep.tile([P, DVE_STAT_TILES, N_CHUNKS, BN_STATS_DIM], F32)
+        diagonal = keep.tile([P, PE_STAT_TILES, P], F32)
+        sum_of_squares = keep.tile([P, PE_STAT_TILES], F32)
+        sum_of_values = keep.tile([P, PE_STAT_TILES], F32)
+        mean_squared = keep.tile([P, PE_STAT_TILES], F32)
+        mean_var = keep.tile([P, CH_TILES, 2], F32)
+        mean = mean_var[:, :, 0]
+        var = mean_var[:, :, 1]
+        std = keep.tile([P, CH_TILES], F32)
+        inv_std = keep.tile([P, CH_TILES], F32)
+        bn_scale = keep.tile([P, CH_TILES], F32)
+        scaled_mean = keep.tile([P, CH_TILES], F32)
+        bn_shift = keep.tile([P, CH_TILES], F32)
+
+        with ExitStack() as part1:
+            w_stage = part1.enter_context(tc.tile_pool(name="w_stage", bufs=1))
+            natural = part1.enter_context(tc.tile_pool(name="natural", bufs=NATURAL_BUFS))
+            sums_psum = part1.enter_context(tc.psum_pool(name="sums_psum", bufs=1))
+            turned = part1.enter_context(tc.psum_pool(name="turned", bufs=PSUM_BANKS - PE_STAT_TILES - 1))
+            squares = [sums_psum.tile([P, P], F32, name="squares%d" % s) for s in range(PE_STAT_TILES)]
+            values = sums_psum.tile([P, PE_STAT_TILES, N_CHUNKS * SUB, 2], F32)
+
+            sources = [ag_chunks[c] for c in range(N_CHUNKS)] + [feat_chunks[c] for c in range(N_CHUNKS)]
+            loaded = []
+
+            def load_next_chunk():
+                if len(loaded) < len(sources):
+                    chunk = natural.tile([P, SUB, CHANNELS], BF16, tag="natural", name="chunk")
+                    nc.sync.dma_start(out=chunk[:], in_=sources[len(loaded)])
+                    loaded.append(chunk)
+
+            for k in range(NATURAL_BUFS):
+                load_next_chunk()
+
+            w_rows = []
+            for w, weight in enumerate((W_feat, W_ag)):
+                w_raw = w_stage.tile([P, PASSES, PACK * COUT], BF16, name="w_raw%d" % w)
+                nc.sync.dma_start(out=w_raw[:], in_=weight.rearrange("(g p t) n -> p g (t n)", p=P, t=PACK))
+                w_rows.append(w_raw[:].rearrange("p g (t n) -> p (g t) n", t=PACK))
+            w_grouped = w_stage.tile([P, 2, PASSES, COUT, PACK], BF16, align_bytes=64)
+            for w in range(2):
+                for g in range(PASSES):
+                    nc.gpsimd.tensor_scalar(
+                        out=by_runs_dst(w_grouped[:, w, g, :, :]),
+                        in0=by_runs_src(w_rows[w][:, g * PACK : (g + 1) * PACK, :]),
+                        scalar1=1.0,
+                        scalar2=0.0,
+                        op0=ALU.mult,
+                        op1=ALU.add,
+                    )
+
+            for c in range(N_CHUNKS):
+                ag_nat = loaded[c]
+                columns = slice(c * CHUNK, (c + 1) * CHUNK)
+                for j in range(CH_TILES):
+                    g, t = divmod(j, PACK)
+                    blocks = [ag_nat[:, i, g * K_PASS + t : (g + 1) * K_PASS : PACK] for i in range(SUB)]
+                    bank = turned.tile([P, SUB, P], BF16, tag="bank")
+                    for i in range(SUB):
+                        nc.tensor.transpose(bank[:, i, :], blocks[i], ident_bf16[:])
+                    nc.scalar.copy(
+                        out=ag_t[:, j, columns].bitcast(F32), in_=bank[:].rearrange("p i q -> p (i q)").bitcast(F32)
+                    )
+                    if j < DVE_STAT_TILES:
+                        nc.vector.bn_stats(out=stats[:, j, c, :], in_=ag_t[:, j, columns])
+                    else:
+                        s = j - DVE_STAT_TILES
+                        for i in range(SUB):
+                            nc.tensor.matmul(
+                                out=squares[s][:],
+                                lhsT=blocks[i],
+                                rhs=blocks[i],
+                                start=(c == 0 and i == 0),
+                                stop=(c == N_CHUNKS - 1 and i == SUB - 1),
+                            )
+                            nc.tensor.matmul(
+                                out=values[:, s, c * SUB + i, :], lhsT=blocks[i], rhs=ones[:, 0:2], start=True, stop=True
+                            )
+                load_next_chunk()
+
+            vector_cols = turned.tile([P, PACK, P], BF16, tag="bank")
+            for t in range(PACK):
+                nc.tensor.transpose(vector_cols[:, t, :], vector_rows[:, t::PACK], ident_bf16[:])
+            nc.scalar.copy(
+                out=gain_shift[:].rearrange("p (r t) -> p r t", t=PACK),
+                in_=vector_cols[:, :, 0 : 2 * PASSES].rearrange("p t r -> p r t"),
+            )
+            bias_sum = turned.tile([P, COUT], F32, tag="bank")
+            nc.tensor.matmul(out=bias_sum[:], lhsT=ones[:], rhs=bias_rows[:], start=True, stop=True)
+            nc.scalar.copy(out=bias[:], in_=bias_sum[:])
+
+            def transpose_feat(c):
+                feat_words = loaded[N_CHUNKS + c][:].bitcast(F32)
+                for g in range(PASSES):
+                    for i0 in range(0, SUB, 2):
+                        bank = turned.tile([P, 2, 2, P], F32, tag="bank")
+                        for u in range(2):
+                            for ii in range(2):
+                                first = 2 * g * P
+                                nc.tensor.transpose(
+                                    bank[:, u, ii, :],
+                                    feat_words[:, i0 + ii, first + u : first + 2 * P : 2],
+                                    ident_f32[:],
+                                )
+                        nc.scalar.copy(
+                            out=feat_grouped_words[:, c, g, i0 * P * 2 : (i0 + 2) * P * 2].rearrange(
+                                "p (q u) -> p q u", u=2
+                            ),
+                            in_=bank[:].rearrange("p u i q -> p (i q) u"),
+                        )
+                load_next_chunk()
+
+            for c in range(FEAT_EARLY):
+                transpose_feat(c)
+
+            for s in range(PE_STAT_TILES):
+                nc.vector.tensor_tensor(out=diagonal[:, s, :], in0=squares[s][:], in1=ident_f32[:], op=ALU.mult)
+            nc.vector.tensor_reduce(out=sum_of_squares[:], in_=diagonal[:], axis=AXIS.X, op=ALU.add)
+            nc.vector.tensor_reduce(out=sum_of_values[:], in_=values[:, :, :, 0], axis=AXIS.X, op=ALU.add)
+            pe_mean = mean_var[:, DVE_STAT_TILES:CH_TILES, 0]
+            pe_var = mean_var[:, DVE_STAT_TILES:CH_TILES, 1]
+            nc.vector.tensor_scalar_mul(out=pe_mean, in0=sum_of_values[:], scalar1=1.0 / POINTS)
+            nc.vector.tensor_mul(out=mean_squared[:], in0=pe_mean, in1=pe_mean)
+            nc.vector.scalar_tensor_tensor(
+                out=pe_var, in0=sum_of_squares[:], scalar=1.0 / POINTS, in1=mean_squared[:], op0=ALU.mult, op1=ALU.subtract
+            )
+            nc.vector.tensor_scalar_max(out=pe_var, in0=pe_var, scalar1=0.0)
+            for j in range(DVE_STAT_TILES):
+                nc.vector.bn_aggr(out=mean_var[:, j, :], in_=stats[:, j, :, :].rearrange("p c s -> p (c s)"))
+
+            nc.scalar.activation(out=std[:], in_=var, func=ACT.Sqrt, bias=eps[:], scale=1.0)
+            for w in range(2):
+                nc.vector.quantize_mx(
+                    out=w_codes[:, w, :, :].rearrange("p g n -> p (g n)").bitcast(FP8X4),
+                    scales=w_scales[:, w, :, :].rearrange("p g n -> p (g n)"),
+                    in_=w_grouped[:, w, :, :, :].rearrange("p g n t -> p (g n t)"),
+                )
+            nc.vector.reciprocal(out=inv_std[:], in_=std[:])
+            nc.vector.tensor_mul(out=bn_scale[:], in0=gain, in1=inv_std[:])
+            nc.vector.tensor_mul(out=scaled_mean[:], in0=mean, in1=bn_scale[:])
+            nc.vector.tensor_sub(out=bn_shift[:], in0=shift, in1=scaled_mean[:])
+
+            for j in range(CH_TILES):
+                nc.vector.tensor_scalar(
+                    out=ag_t[:, j, :],
+                    in0=ag_t[:, j, :],
+                    scalar1=bn_scale[:, j : j + 1],
+                    scalar2=bn_shift[:, j : j + 1],
+                    op0=ALU.mult,
+                    op1=ALU.add,
+                )
+
+            for c in range(FEAT_EARLY, N_CHUNKS):
+                transpose_feat(c)
+
+        with ExitStack() as part2:
+            stage = part2.enter_context(tc.tile_pool(name="stage", bufs=2, reuse_waits="tile"))
+            codes_pool = part2.enter_context(tc.tile_pool(name="codes", bufs=3, reuse_waits="tile"))
+            psum = part2.enter_context(tc.psum_pool(name="psum", bufs=PSUM_BANKS, reuse_waits="tile"))
+            h_grouped = {}
+            operands = {}
+            products = {}
+
+            def relu_and_regroup(c):
+                columns = slice(c * CHUNK, (c + 1) * CHUNK)
+                h_grouped[c] = stage.tile([P, PASSES, CHUNK, PACK], BF16, align_bytes=64, name="h_grouped")
+                for g in range(PASSES):
+                    grouped = by_runs_dst(h_grouped[c][:, g, :, :])
+                    rows = by_runs_src(ag_t[:, g * PACK : (g + 1) * PACK, columns])
+                    if g == PASSES - 1 and c % VECTOR_REGROUPS_EVERY == VECTOR_REGROUPS_EVERY - 1:
+                        nc.vector.tensor_scalar_max(out=grouped, in0=rows, scalar1=0.0)
+                    else:
+                        nc.scalar.activation(out=grouped, in_=rows, func=ACT.Relu)
+
+            def quantise_feat(c):
+                feat_codes = codes_pool.tile([P, PASSES, CHUNK], U32, align_bytes=64, bufs=FEAT_AHEAD + 2)
+                feat_scales = codes_pool.tile([P, PASSES, CHUNK], U8, align_bytes=64, bufs=FEAT_AHEAD + 2)
+                nc.vector.quantize_mx(
+                    out=feat_codes[:].rearrange("p g q -> p (g q)").bitcast(FP8X4),
+                    scales=feat_scales[:].rearrange("p g q -> p (g q)"),
+                    in_=feat_grouped[:, c, :, :].rearrange("p g x -> p (g x)"),
+                )
+                operands[c] = [(feat_codes, feat_scales)]
+
+            def quantise_h(c):
+                h_codes = codes_pool.tile([P, PASSES, CHUNK], U32, align_bytes=64)
+                h_scales = codes_pool.tile([P, PASSES, CHUNK], U8, align_bytes=64)
+                for g in range(PASSES):
+                    nc.vector.quantize_mx(
+                        out=h_codes[:, g, :].bitcast(FP8X4),
+                        scales=h_scales[:, g, :],
+                        in_=h_grouped[c][:, g, :, :].rearrange("p q t -> p (q t)"),
+                    )
+                operands[c].append((h_codes, h_scales))
+
+            def multiply(c):
+                products[c] = [psum.tile([P, COUT], F32, tag="bank", name="product") for i in range(SUB)]
+                for w in range(2):
+                    codes, scales = operands[c][w]
+                    for g in range(PASSES):
+                        for i in range(SUB):
+                            points = slice(i * P, (i + 1) * P)
+                            nc.tensor.matmul_mx(
+                                out=products[c][i][:],
+                                lhsT=codes[:, g, points].bitcast(FP8X4),
+                                lhsT_scale=scales[:, g, points],
+                                rhs=w_codes[:, w, g, :].bitcast(FP8X4),
+                                rhs_scale=w_scales[:, w, g, :],
+                                start=(w == 0 and g == 0),
+                                stop=(w == 1 and g == PASSES - 1),
+                            )
+
+            def add_bias_and_store(c):
+                result = stage.tile([P, SUB, COUT], F32)
+                for i in range(SUB):
+                    nc.vector.tensor_tensor(out=result[:, i, :], in0=products[c][i][:], in1=bias[:], op=ALU.add)
+                    nc.sync.dma_start(out=out_chunks[c][:, i, :], in_=result[:, i, :])
+
+            for c in range(FEAT_AHEAD - 1):
+                quantise_feat(c)
+            for k in range(-1, N_CHUNKS + 1):
+                if k + 1 < N_CHUNKS:
+                    relu_and_regroup(k + 1)
+                if k + FEAT_AHEAD < N_CHUNKS:
+                    quantise_feat(k + FEAT_AHEAD)
+                if 0 <= k < N_CHUNKS:
+                    quantise_h(k)
+                    multiply(k)
+                if 0 <= k - 1:
+                    add_bias_and_store(k - 1)

@@ -31,8 +31,9 @@ PSUM_BANKS = 8
 NATURAL_BUFS = 5
 PE_STAT_TILES = 3
 DVE_STAT_TILES = CH_TILES - PE_STAT_TILES
-FEAT_EARLY = 2
-FEAT_AHEAD = 3
+TURN_BANKS = SUB
+PRODUCT_BANKS = PSUM_BANKS - TURN_BANKS
+FEAT_TURN_AHEAD = 3
 VECTOR_REGROUPS_EVERY = 4
 RUN = 4
 
@@ -56,6 +57,10 @@ def tile_geoconv_pb_t_kernel(tc, feat, ag, W_feat, b_feat, g1, be1, W_ag, b_ag, 
     with ExitStack() as ctx:
         ctx.enter_context(tc.manual_schedule())
         keep = ctx.enter_context(tc.tile_pool(name="keep", bufs=1))
+        feat_pool = ctx.enter_context(tc.tile_pool(name="feat_pool", bufs=3))
+        h_pool = ctx.enter_context(tc.tile_pool(name="h_pool", bufs=2))
+        natural = ctx.enter_context(tc.tile_pool(name="natural", bufs=NATURAL_BUFS, side="right"))
+        turned = ctx.enter_context(tc.psum_pool(name="turned", bufs=TURN_BANKS))
 
         ident_bf16 = keep.tile([P, P], BF16)
         make_identity(nc, ident_bf16[:])
@@ -82,14 +87,12 @@ def tile_geoconv_pb_t_kernel(tc, feat, ag, W_feat, b_feat, g1, be1, W_ag, b_ag, 
         shift = gain_shift[:, CH_TILES : 2 * CH_TILES]
         bias = keep.tile([P, COUT], F32)
 
-        ag_t = keep.tile([P, CH_TILES, POINTS], BF16)
-        feat_grouped = keep.tile([P, N_CHUNKS, PASSES, CHUNK * PACK], BF16, align_bytes=64)
-        feat_grouped_words = feat_grouped[:].bitcast(F32)
+        ag_t = [keep.tile([P, CH_TILES, CHUNK], BF16, name="ag_t%d" % c) for c in range(N_CHUNKS)]
         w_codes = keep.tile([P, 2, PASSES, COUT], U32, align_bytes=64)
         w_scales = keep.tile([P, 2, PASSES, COUT], U8, align_bytes=64)
         stats = keep.tile([P, DVE_STAT_TILES, N_CHUNKS, BN_STATS_DIM], F32)
         diagonal = keep.tile([P, PE_STAT_TILES, P], F32)
-        sum_of_squares = keep.tile([P, PE_STAT_TILES], F32)
+        mean_of_squares = keep.tile([P, PE_STAT_TILES], F32)
         sum_of_values = keep.tile([P, PE_STAT_TILES], F32)
         mean_squared = keep.tile([P, PE_STAT_TILES], F32)
         mean_var = keep.tile([P, CH_TILES, 2], F32)
@@ -101,31 +104,109 @@ def tile_geoconv_pb_t_kernel(tc, feat, ag, W_feat, b_feat, g1, be1, W_ag, b_ag, 
         scaled_mean = keep.tile([P, CH_TILES], F32)
         bn_shift = keep.tile([P, CH_TILES], F32)
 
+        sources = [ag_chunks[c] for c in range(N_CHUNKS)] + [feat_chunks[c] for c in range(N_CHUNKS)]
+        loaded = []
+
+        def load_next_chunk():
+            if len(loaded) < len(sources):
+                chunk = natural.tile([P, SUB, CHANNELS], BF16, tag="natural", name="chunk")
+                pieces = PASSES if not loaded else 1
+                for piece in range(pieces):
+                    channels = slice(piece * CHANNELS // pieces, (piece + 1) * CHANNELS // pieces)
+                    nc.sync.dma_start(out=chunk[:, :, channels], in_=sources[len(loaded)][:, :, channels])
+                loaded.append(chunk)
+
+        feat_grouped = {}
+        feat_operands = {}
+        h_grouped = {}
+        h_operands = {}
+        products = {}
+
+        def transpose_feat(c):
+            feat_words = loaded[N_CHUNKS + c][:].bitcast(F32)
+            feat_grouped[c] = feat_pool.tile([P, PASSES, CHUNK * PACK], BF16, align_bytes=64, bufs=4, name="feat_grouped")
+            grouped_words = feat_grouped[c][:].bitcast(F32)
+            for g in range(PASSES):
+                for i0 in range(0, SUB, 2):
+                    bank = turned.tile([P, 2, 2, P], F32, tag="bank")
+                    for u in range(2):
+                        for ii in range(2):
+                            first = 2 * g * P
+                            nc.tensor.transpose(
+                                bank[:, u, ii, :],
+                                feat_words[:, i0 + ii, first + u : first + 2 * P : 2],
+                                ident_f32[:],
+                            )
+                    nc.scalar.copy(
+                        out=grouped_words[:, g, i0 * P * 2 : (i0 + 2) * P * 2].rearrange("p (q u) -> p q u", u=2),
+                        in_=bank[:].rearrange("p u i q -> p (i q) u"),
+                    )
+            load_next_chunk()
+
+        def quantise_feat(c):
+            feat_codes = feat_pool.tile([P, PASSES, CHUNK], U32, align_bytes=64)
+            feat_scales = feat_pool.tile([P, PASSES, CHUNK], U8, align_bytes=64)
+            nc.vector.quantize_mx(
+                out=feat_codes[:].rearrange("p g q -> p (g q)").bitcast(FP8X4),
+                scales=feat_scales[:].rearrange("p g q -> p (g q)"),
+                in_=feat_grouped[c][:].rearrange("p g x -> p (g x)"),
+            )
+            feat_operands[c] = (feat_codes, feat_scales)
+
+        def batch_norm(c):
+            for j in range(CH_TILES):
+                nc.vector.tensor_scalar(
+                    out=ag_t[c][:, j, :],
+                    in0=ag_t[c][:, j, :],
+                    scalar1=bn_scale[:, j : j + 1],
+                    scalar2=bn_shift[:, j : j + 1],
+                    op0=ALU.mult,
+                    op1=ALU.add,
+                )
+
+        def relu_and_regroup(c, g, on_vector):
+            if c not in h_grouped:
+                h_grouped[c] = h_pool.tile([P, PASSES, CHUNK, PACK], BF16, align_bytes=64, name="h_grouped")
+            grouped = by_runs_dst(h_grouped[c][:, g, :, :])
+            rows = by_runs_src(ag_t[c][:, g * PACK : (g + 1) * PACK, :])
+            if on_vector:
+                nc.vector.tensor_scalar_max(out=grouped, in0=rows, scalar1=0.0)
+            else:
+                nc.scalar.activation(out=grouped, in_=rows, func=ACT.Relu)
+
+        def vector_regroups(c, g):
+            return g == PASSES - 1 and c % VECTOR_REGROUPS_EVERY == 0
+
+        def quantise_h(c):
+            h_codes = h_pool.tile([P, PASSES, CHUNK], U32, align_bytes=64)
+            h_scales = h_pool.tile([P, PASSES, CHUNK], U8, align_bytes=64)
+            for g in range(PASSES):
+                nc.vector.quantize_mx(
+                    out=h_codes[:, g, :].bitcast(FP8X4),
+                    scales=h_scales[:, g, :],
+                    in_=h_grouped[c][:, g, :, :].rearrange("p q t -> p (q t)"),
+                )
+            h_operands[c] = (h_codes, h_scales)
+
         with ExitStack() as part1:
             w_stage = part1.enter_context(tc.tile_pool(name="w_stage", bufs=1))
-            natural = part1.enter_context(tc.tile_pool(name="natural", bufs=NATURAL_BUFS))
             sums_psum = part1.enter_context(tc.psum_pool(name="sums_psum", bufs=1))
-            turned = part1.enter_context(tc.psum_pool(name="turned", bufs=PSUM_BANKS - PE_STAT_TILES - 1))
             squares = [sums_psum.tile([P, P], F32, name="squares%d" % s) for s in range(PE_STAT_TILES)]
             values = sums_psum.tile([P, PE_STAT_TILES, N_CHUNKS * SUB, 2], F32)
 
-            sources = [ag_chunks[c] for c in range(N_CHUNKS)] + [feat_chunks[c] for c in range(N_CHUNKS)]
-            loaded = []
-
-            def load_next_chunk():
-                if len(loaded) < len(sources):
-                    chunk = natural.tile([P, SUB, CHANNELS], BF16, tag="natural", name="chunk")
-                    nc.sync.dma_start(out=chunk[:], in_=sources[len(loaded)])
-                    loaded.append(chunk)
-
-            for k in range(NATURAL_BUFS):
-                load_next_chunk()
-
             w_rows = []
-            for w, weight in enumerate((W_feat, W_ag)):
+
+            def load_weight(w, weight):
                 w_raw = w_stage.tile([P, PASSES, PACK * COUT], BF16, name="w_raw%d" % w)
                 nc.sync.dma_start(out=w_raw[:], in_=weight.rearrange("(g p t) n -> p g (t n)", p=P, t=PACK))
                 w_rows.append(w_raw[:].rearrange("p g (t n) -> p (g t) n", t=PACK))
+
+            for k in range(NATURAL_BUFS - 2):
+                load_next_chunk()
+            load_weight(0, W_feat)
+            for k in range(2):
+                load_next_chunk()
+            load_weight(1, W_ag)
             w_grouped = w_stage.tile([P, 2, PASSES, COUT, PACK], BF16, align_bytes=64)
             for w in range(2):
                 for g in range(PASSES):
@@ -140,7 +221,6 @@ def tile_geoconv_pb_t_kernel(tc, feat, ag, W_feat, b_feat, g1, be1, W_ag, b_ag, 
 
             for c in range(N_CHUNKS):
                 ag_nat = loaded[c]
-                columns = slice(c * CHUNK, (c + 1) * CHUNK)
                 for j in range(CH_TILES):
                     g, t = divmod(j, PACK)
                     blocks = [ag_nat[:, i, g * K_PASS + t : (g + 1) * K_PASS : PACK] for i in range(SUB)]
@@ -148,10 +228,10 @@ def tile_geoconv_pb_t_kernel(tc, feat, ag, W_feat, b_feat, g1, be1, W_ag, b_ag, 
                     for i in range(SUB):
                         nc.tensor.transpose(bank[:, i, :], blocks[i], ident_bf16[:])
                     nc.scalar.copy(
-                        out=ag_t[:, j, columns].bitcast(F32), in_=bank[:].rearrange("p i q -> p (i q)").bitcast(F32)
+                        out=ag_t[c][:, j, :].bitcast(F32), in_=bank[:].rearrange("p i q -> p (i q)").bitcast(F32)
                     )
                     if j < DVE_STAT_TILES:
-                        nc.vector.bn_stats(out=stats[:, j, c, :], in_=ag_t[:, j, columns])
+                        nc.vector.bn_stats(out=stats[:, j, c, :], in_=ag_t[c][:, j, :])
                     else:
                         s = j - DVE_STAT_TILES
                         for i in range(SUB):
@@ -178,142 +258,92 @@ def tile_geoconv_pb_t_kernel(tc, feat, ag, W_feat, b_feat, g1, be1, W_ag, b_ag, 
             nc.tensor.matmul(out=bias_sum[:], lhsT=ones[:], rhs=bias_rows[:], start=True, stop=True)
             nc.scalar.copy(out=bias[:], in_=bias_sum[:])
 
-            def transpose_feat(c):
-                feat_words = loaded[N_CHUNKS + c][:].bitcast(F32)
-                for g in range(PASSES):
-                    for i0 in range(0, SUB, 2):
-                        bank = turned.tile([P, 2, 2, P], F32, tag="bank")
-                        for u in range(2):
-                            for ii in range(2):
-                                first = 2 * g * P
-                                nc.tensor.transpose(
-                                    bank[:, u, ii, :],
-                                    feat_words[:, i0 + ii, first + u : first + 2 * P : 2],
-                                    ident_f32[:],
-                                )
-                        nc.scalar.copy(
-                            out=feat_grouped_words[:, c, g, i0 * P * 2 : (i0 + 2) * P * 2].rearrange(
-                                "p (q u) -> p q u", u=2
-                            ),
-                            in_=bank[:].rearrange("p u i q -> p (i q) u"),
-                        )
-                load_next_chunk()
-
-            for c in range(FEAT_EARLY):
-                transpose_feat(c)
+            transpose_feat(0)
 
             for s in range(PE_STAT_TILES):
-                nc.vector.tensor_tensor(out=diagonal[:, s, :], in0=squares[s][:], in1=ident_f32[:], op=ALU.mult)
-            nc.vector.tensor_reduce(out=sum_of_squares[:], in_=diagonal[:], axis=AXIS.X, op=ALU.add)
+                nc.vector.scalar_tensor_tensor(
+                    out=diagonal[:, s, :],
+                    in0=squares[s][:],
+                    scalar=1.0 / POINTS,
+                    in1=ident_f32[:],
+                    op0=ALU.mult,
+                    op1=ALU.mult,
+                    accum_out=mean_of_squares[:, s : s + 1],
+                )
             nc.vector.tensor_reduce(out=sum_of_values[:], in_=values[:, :, :, 0], axis=AXIS.X, op=ALU.add)
             pe_mean = mean_var[:, DVE_STAT_TILES:CH_TILES, 0]
             pe_var = mean_var[:, DVE_STAT_TILES:CH_TILES, 1]
-            nc.vector.tensor_scalar_mul(out=pe_mean, in0=sum_of_values[:], scalar1=1.0 / POINTS)
-            nc.vector.tensor_mul(out=mean_squared[:], in0=pe_mean, in1=pe_mean)
-            nc.vector.scalar_tensor_tensor(
-                out=pe_var, in0=sum_of_squares[:], scalar=1.0 / POINTS, in1=mean_squared[:], op0=ALU.mult, op1=ALU.subtract
-            )
-            nc.vector.tensor_scalar_max(out=pe_var, in0=pe_var, scalar1=0.0)
+            chain = [
+                lambda: nc.vector.tensor_scalar_mul(out=pe_mean, in0=sum_of_values[:], scalar1=1.0 / POINTS),
+                lambda: nc.vector.tensor_mul(out=mean_squared[:], in0=pe_mean, in1=pe_mean),
+                lambda: nc.vector.tensor_sub(out=pe_var, in0=mean_of_squares[:], in1=mean_squared[:]),
+                lambda: nc.vector.tensor_scalar_max(out=pe_var, in0=pe_var, scalar1=0.0),
+            ]
             for j in range(DVE_STAT_TILES):
                 nc.vector.bn_aggr(out=mean_var[:, j, :], in_=stats[:, j, :, :].rearrange("p c s -> p (c s)"))
+                if j < len(chain):
+                    chain[j]()
 
             nc.scalar.activation(out=std[:], in_=var, func=ACT.Sqrt, bias=eps[:], scale=1.0)
+            nc.vector.reciprocal(out=inv_std[:], in_=std[:])
+            nc.vector.tensor_mul(out=bn_scale[:], in0=gain, in1=inv_std[:])
+            nc.vector.tensor_mul(out=scaled_mean[:], in0=mean, in1=bn_scale[:])
+            nc.vector.tensor_sub(out=bn_shift[:], in0=shift, in1=scaled_mean[:])
+
+            transpose_feat(1)
+            batch_norm(0)
+            for g in range(PASSES):
+                relu_and_regroup(0, g, vector_regroups(0, g))
+            transpose_feat(2)
+            batch_norm(1)
             for w in range(2):
                 nc.vector.quantize_mx(
                     out=w_codes[:, w, :, :].rearrange("p g n -> p (g n)").bitcast(FP8X4),
                     scales=w_scales[:, w, :, :].rearrange("p g n -> p (g n)"),
                     in_=w_grouped[:, w, :, :, :].rearrange("p g n t -> p (g n t)"),
                 )
-            nc.vector.reciprocal(out=inv_std[:], in_=std[:])
-            nc.vector.tensor_mul(out=bn_scale[:], in0=gain, in1=inv_std[:])
-            nc.vector.tensor_mul(out=scaled_mean[:], in0=mean, in1=bn_scale[:])
-            nc.vector.tensor_sub(out=bn_shift[:], in0=shift, in1=scaled_mean[:])
+            quantise_feat(0)
 
-            for j in range(CH_TILES):
-                nc.vector.tensor_scalar(
-                    out=ag_t[:, j, :],
-                    in0=ag_t[:, j, :],
-                    scalar1=bn_scale[:, j : j + 1],
-                    scalar2=bn_shift[:, j : j + 1],
-                    op0=ALU.mult,
-                    op1=ALU.add,
-                )
+        result_pool = ctx.enter_context(tc.tile_pool(name="result_pool", bufs=8, reuse_waits="tile"))
+        product_psum = ctx.enter_context(tc.psum_pool(name="product_psum", bufs=PRODUCT_BANKS, reuse_waits="tile"))
 
-            for c in range(FEAT_EARLY, N_CHUNKS):
-                transpose_feat(c)
-
-        with ExitStack() as part2:
-            stage = part2.enter_context(tc.tile_pool(name="stage", bufs=2, reuse_waits="tile"))
-            codes_pool = part2.enter_context(tc.tile_pool(name="codes", bufs=3, reuse_waits="tile"))
-            psum = part2.enter_context(tc.psum_pool(name="psum", bufs=PSUM_BANKS, reuse_waits="tile"))
-            h_grouped = {}
-            operands = {}
-            products = {}
-
-            def relu_and_regroup(c):
-                columns = slice(c * CHUNK, (c + 1) * CHUNK)
-                h_grouped[c] = stage.tile([P, PASSES, CHUNK, PACK], BF16, align_bytes=64, name="h_grouped")
-                for g in range(PASSES):
-                    grouped = by_runs_dst(h_grouped[c][:, g, :, :])
-                    rows = by_runs_src(ag_t[:, g * PACK : (g + 1) * PACK, columns])
-                    if g == PASSES - 1 and c % VECTOR_REGROUPS_EVERY == VECTOR_REGROUPS_EVERY - 1:
-                        nc.vector.tensor_scalar_max(out=grouped, in0=rows, scalar1=0.0)
-                    else:
-                        nc.scalar.activation(out=grouped, in_=rows, func=ACT.Relu)
-
-            def quantise_feat(c):
-                feat_codes = codes_pool.tile([P, PASSES, CHUNK], U32, align_bytes=64, bufs=FEAT_AHEAD + 2)
-                feat_scales = codes_pool.tile([P, PASSES, CHUNK], U8, align_bytes=64, bufs=FEAT_AHEAD + 2)
-                nc.vector.quantize_mx(
-                    out=feat_codes[:].rearrange("p g q -> p (g q)").bitcast(FP8X4),
-                    scales=feat_scales[:].rearrange("p g q -> p (g q)"),
-                    in_=feat_grouped[:, c, :, :].rearrange("p g x -> p (g x)"),
-                )
-                operands[c] = [(feat_codes, feat_scales)]
-
-            def quantise_h(c):
-                h_codes = codes_pool.tile([P, PASSES, CHUNK], U32, align_bytes=64)
-                h_scales = codes_pool.tile([P, PASSES, CHUNK], U8, align_bytes=64)
-                for g in range(PASSES):
-                    nc.vector.quantize_mx(
-                        out=h_codes[:, g, :].bitcast(FP8X4),
-                        scales=h_scales[:, g, :],
-                        in_=h_grouped[c][:, g, :, :].rearrange("p q t -> p (q t)"),
-                    )
-                operands[c].append((h_codes, h_scales))
-
-            def multiply(c):
-                products[c] = [psum.tile([P, COUT], F32, tag="bank", name="product") for i in range(SUB)]
-                for w in range(2):
-                    codes, scales = operands[c][w]
+        def multiply(c):
+            for i in range(SUB):
+                points = slice(i * P, (i + 1) * P)
+                product = product_psum.tile([P, COUT], F32, tag="bank", name="product")
+                for w, (codes, scales) in enumerate((feat_operands[c], h_operands[c])):
                     for g in range(PASSES):
-                        for i in range(SUB):
-                            points = slice(i * P, (i + 1) * P)
-                            nc.tensor.matmul_mx(
-                                out=products[c][i][:],
-                                lhsT=codes[:, g, points].bitcast(FP8X4),
-                                lhsT_scale=scales[:, g, points],
-                                rhs=w_codes[:, w, g, :].bitcast(FP8X4),
-                                rhs_scale=w_scales[:, w, g, :],
-                                start=(w == 0 and g == 0),
-                                stop=(w == 1 and g == PASSES - 1),
-                            )
+                        nc.tensor.matmul_mx(
+                            out=product[:],
+                            lhsT=codes[:, g, points].bitcast(FP8X4),
+                            lhsT_scale=scales[:, g, points],
+                            rhs=w_codes[:, w, g, :].bitcast(FP8X4),
+                            rhs_scale=w_scales[:, w, g, :],
+                            start=(w == 0 and g == 0),
+                            stop=(w == 1 and g == PASSES - 1),
+                        )
+                products[c, i] = product
 
-            def add_bias_and_store(c):
-                result = stage.tile([P, SUB, COUT], F32)
-                for i in range(SUB):
-                    nc.vector.tensor_tensor(out=result[:, i, :], in0=products[c][i][:], in1=bias[:], op=ALU.add)
-                    nc.sync.dma_start(out=out_chunks[c][:, i, :], in_=result[:, i, :])
+        def add_bias_and_store(c, sub_tiles):
+            for i in sub_tiles:
+                result = result_pool.tile([P, COUT], F32)
+                nc.vector.tensor_tensor(out=result[:], in0=products[c, i][:], in1=bias[:], op=ALU.add)
+                nc.sync.dma_start(out=out_chunks[c][:, i, :], in_=result[:])
 
-            for c in range(FEAT_AHEAD - 1):
-                quantise_feat(c)
-            for k in range(-1, N_CHUNKS + 1):
-                if k + 1 < N_CHUNKS:
-                    relu_and_regroup(k + 1)
-                if k + FEAT_AHEAD < N_CHUNKS:
-                    quantise_feat(k + FEAT_AHEAD)
-                if 0 <= k < N_CHUNKS:
-                    quantise_h(k)
-                    multiply(k)
-                if 0 <= k - 1:
-                    add_bias_and_store(k - 1)
+        first_half = range(SUB // 2)
+        second_half = range(SUB // 2, SUB)
+        for c in range(N_CHUNKS):
+            quantise_h(c)
+            if c > 0:
+                add_bias_and_store(c - 1, second_half)
+            if c + FEAT_TURN_AHEAD < N_CHUNKS:
+                transpose_feat(c + FEAT_TURN_AHEAD)
+            multiply(c)
+            if c + 2 < N_CHUNKS:
+                batch_norm(c + 2)
+            if c + 1 < N_CHUNKS:
+                for g in range(PASSES):
+                    relu_and_regroup(c + 1, g, vector_regroups(c + 1, g))
+                quantise_feat(c + 1)
+            add_bias_and_store(c, first_half)
+        add_bias_and_store(N_CHUNKS - 1, second_half)

@@ -29,11 +29,11 @@ CH_TILES = CHANNELS // P
 BN_STATS_DIM = 6
 PSUM_BANKS = 8
 NATURAL_BUFS = 5
-PE_STAT_TILES = 3
-DVE_STAT_TILES = CH_TILES - PE_STAT_TILES
-TURN_BANKS = SUB
+DVE_STAT_TILES = PACK
+PE_STAT_TILES = PACK
+TURN_BANKS = PSUM_BANKS - PE_STAT_TILES - 1
 PRODUCT_BANKS = PSUM_BANKS - TURN_BANKS
-FEAT_TURN_AHEAD = 3
+FEAT_TURN_AHEAD = 2
 VECTOR_REGROUPS_EVERY = 4
 RUN = 4
 
@@ -82,12 +82,30 @@ def tile_geoconv_pb_t_kernel(tc, feat, ag, W_feat, b_feat, g1, be1, W_ag, b_ag, 
         nc.vector.memset(bias_rows[:], 0.0)
         nc.scalar.dma_start(out=bias_rows[0:1, :], in_=b_feat.rearrange("(o n) -> o n", o=1))
         nc.scalar.dma_start(out=bias_rows[1:2, :], in_=b_ag.rearrange("(o n) -> o n", o=1))
-        gain_shift = keep.tile([P, 2 * CH_TILES], F32)
-        gain = gain_shift[:, 0:CH_TILES]
-        shift = gain_shift[:, CH_TILES : 2 * CH_TILES]
+        gain_shift = keep.tile([P, 2, CH_TILES], F32)
+        gain = gain_shift[:, 0, :]
+        shift = gain_shift[:, 1, :]
+        select = keep.tile([P, PACK, PACK, P // PACK], F32)
+        for q in range(PACK):
+            nc.gpsimd.tensor_scalar(
+                out=select[:, :, q, :],
+                in0=ident_f32[:].rearrange("p (c t) -> p t c", t=PACK),
+                scalar1=1.0,
+                scalar2=0.0,
+                op0=ALU.mult,
+                op1=ALU.add,
+            )
+        quarter = keep.tile([P, PACK], F32)
+        nc.vector.tensor_reduce(
+            out=quarter[:], in_=ident_f32[:].rearrange("p (q c) -> p q c", q=PACK), axis=AXIS.X, op=ALU.add
+        )
         bias = keep.tile([P, COUT], F32)
 
-        ag_t = [keep.tile([P, CH_TILES, CHUNK], BF16, name="ag_t%d" % c) for c in range(N_CHUNKS)]
+        ag_words = [keep.tile([P, 2 * PASSES, CHUNK], F32, name="ag_words%d" % c) for c in range(N_CHUNKS)]
+
+        def ag_values(c, j):
+            return ag_words[c][:, j // 2, :].bitcast(BF16)[:, j % 2 :: 2]
+
         w_codes = keep.tile([P, 2, PASSES, COUT], U32, align_bytes=64)
         w_scales = keep.tile([P, 2, PASSES, COUT], U8, align_bytes=64)
         stats = keep.tile([P, DVE_STAT_TILES, N_CHUNKS, BN_STATS_DIM], F32)
@@ -100,12 +118,16 @@ def tile_geoconv_pb_t_kernel(tc, feat, ag, W_feat, b_feat, g1, be1, W_ag, b_ag, 
         var = mean_var[:, :, 1]
         std = keep.tile([P, CH_TILES], F32)
         inv_std = keep.tile([P, CH_TILES], F32)
-        bn_scale = keep.tile([P, CH_TILES], F32)
+        scale_shift = keep.tile([P, 2, CH_TILES], F32)
         scaled_mean = keep.tile([P, CH_TILES], F32)
-        bn_shift = keep.tile([P, CH_TILES], F32)
+        masked = keep.tile([P, PACK * 2, PACK], F32)
+        scale_shift_1 = keep.tile([P, PACK, 2], F32)
+        bn_scale = [scale_shift[:, 0, t : t + 1] for t in range(PACK)] + [scale_shift_1[:, t, 0:1] for t in range(PACK)]
+        bn_shift = [scale_shift[:, 1, t : t + 1] for t in range(PACK)] + [scale_shift_1[:, t, 1:2] for t in range(PACK)]
 
         sources = [ag_chunks[c] for c in range(N_CHUNKS)] + [feat_chunks[c] for c in range(N_CHUNKS)]
         loaded = []
+        w_rows = []
 
         def load_next_chunk():
             if len(loaded) < len(sources):
@@ -116,15 +138,21 @@ def tile_geoconv_pb_t_kernel(tc, feat, ag, W_feat, b_feat, g1, be1, W_ag, b_ag, 
                     nc.sync.dma_start(out=chunk[:, :, channels], in_=sources[len(loaded)][:, :, channels])
                 loaded.append(chunk)
 
+        def load_weight(weight):
+            w_raw = natural.tile([P, PASSES, PACK * COUT], BF16, tag="natural", name="w_raw")
+            nc.sync.dma_start(out=w_raw[:], in_=weight.rearrange("(g p t) n -> p g (t n)", p=P, t=PACK))
+            w_rows.append(w_raw[:].rearrange("p g (t n) -> p (g t) n", t=PACK))
+
         feat_grouped = {}
         feat_operands = {}
+        h_normed = {}
         h_grouped = {}
         h_operands = {}
         products = {}
 
         def transpose_feat(c):
             feat_words = loaded[N_CHUNKS + c][:].bitcast(F32)
-            feat_grouped[c] = feat_pool.tile([P, PASSES, CHUNK * PACK], BF16, align_bytes=64, bufs=4, name="feat_grouped")
+            feat_grouped[c] = feat_pool.tile([P, PASSES, CHUNK * PACK], BF16, align_bytes=64, name="feat_grouped")
             grouped_words = feat_grouped[c][:].bitcast(F32)
             for g in range(PASSES):
                 for i0 in range(0, SUB, 2):
@@ -153,29 +181,28 @@ def tile_geoconv_pb_t_kernel(tc, feat, ag, W_feat, b_feat, g1, be1, W_ag, b_ag, 
             )
             feat_operands[c] = (feat_codes, feat_scales)
 
-        def batch_norm(c):
-            for j in range(CH_TILES):
+        def batch_norm(c, g):
+            h_normed[c, g] = h_pool.tile([P, PACK, CHUNK], BF16, bufs=4, name="h_normed")
+            for t in range(PACK):
+                j = g * PACK + t
                 nc.vector.tensor_scalar(
-                    out=ag_t[c][:, j, :],
-                    in0=ag_t[c][:, j, :],
-                    scalar1=bn_scale[:, j : j + 1],
-                    scalar2=bn_shift[:, j : j + 1],
+                    out=h_normed[c, g][:, t, :],
+                    in0=ag_values(c, j),
+                    scalar1=bn_scale[j],
+                    scalar2=bn_shift[j],
                     op0=ALU.mult,
                     op1=ALU.add,
                 )
 
-        def relu_and_regroup(c, g, on_vector):
+        def relu_and_regroup(c, g):
             if c not in h_grouped:
                 h_grouped[c] = h_pool.tile([P, PASSES, CHUNK, PACK], BF16, align_bytes=64, name="h_grouped")
             grouped = by_runs_dst(h_grouped[c][:, g, :, :])
-            rows = by_runs_src(ag_t[c][:, g * PACK : (g + 1) * PACK, :])
-            if on_vector:
+            rows = by_runs_src(h_normed[c, g][:])
+            if g == PASSES - 1 and c % VECTOR_REGROUPS_EVERY == 0:
                 nc.vector.tensor_scalar_max(out=grouped, in0=rows, scalar1=0.0)
             else:
                 nc.scalar.activation(out=grouped, in_=rows, func=ACT.Relu)
-
-        def vector_regroups(c, g):
-            return g == PASSES - 1 and c % VECTOR_REGROUPS_EVERY == 0
 
         def quantise_h(c):
             h_codes = h_pool.tile([P, PASSES, CHUNK], U32, align_bytes=64)
@@ -194,21 +221,13 @@ def tile_geoconv_pb_t_kernel(tc, feat, ag, W_feat, b_feat, g1, be1, W_ag, b_ag, 
             squares = [sums_psum.tile([P, P], F32, name="squares%d" % s) for s in range(PE_STAT_TILES)]
             values = sums_psum.tile([P, PE_STAT_TILES, N_CHUNKS * SUB, 2], F32)
 
-            w_rows = []
-
-            def load_weight(w, weight):
-                w_raw = w_stage.tile([P, PASSES, PACK * COUT], BF16, name="w_raw%d" % w)
-                nc.sync.dma_start(out=w_raw[:], in_=weight.rearrange("(g p t) n -> p g (t n)", p=P, t=PACK))
-                w_rows.append(w_raw[:].rearrange("p g (t n) -> p (g t) n", t=PACK))
-
             for k in range(NATURAL_BUFS - 2):
                 load_next_chunk()
-            load_weight(0, W_feat)
-            for k in range(2):
-                load_next_chunk()
-            load_weight(1, W_ag)
+            load_weight(W_feat)
+            load_next_chunk()
             w_grouped = w_stage.tile([P, 2, PASSES, COUT, PACK], BF16, align_bytes=64)
-            for w in range(2):
+
+            def group_weight(w):
                 for g in range(PASSES):
                     nc.gpsimd.tensor_scalar(
                         out=by_runs_dst(w_grouped[:, w, g, :, :]),
@@ -219,41 +238,49 @@ def tile_geoconv_pb_t_kernel(tc, feat, ag, W_feat, b_feat, g1, be1, W_ag, b_ag, 
                         op1=ALU.add,
                     )
 
+            group_weight(0)
             for c in range(N_CHUNKS):
                 ag_nat = loaded[c]
-                for j in range(CH_TILES):
-                    g, t = divmod(j, PACK)
-                    blocks = [ag_nat[:, i, g * K_PASS + t : (g + 1) * K_PASS : PACK] for i in range(SUB)]
-                    bank = turned.tile([P, SUB, P], BF16, tag="bank")
+                nat_words = ag_nat[:].bitcast(F32)
+                for a in range(2 * PASSES):
+                    g, u = divmod(a, 2)
+                    bank = turned.tile([P, SUB, P], F32, tag="bank")
                     for i in range(SUB):
-                        nc.tensor.transpose(bank[:, i, :], blocks[i], ident_bf16[:])
-                    nc.scalar.copy(
-                        out=ag_t[c][:, j, :].bitcast(F32), in_=bank[:].rearrange("p i q -> p (i q)").bitcast(F32)
-                    )
-                    if j < DVE_STAT_TILES:
-                        nc.vector.bn_stats(out=stats[:, j, c, :], in_=ag_t[c][:, j, :])
-                    else:
-                        s = j - DVE_STAT_TILES
-                        for i in range(SUB):
-                            nc.tensor.matmul(
-                                out=squares[s][:],
-                                lhsT=blocks[i],
-                                rhs=blocks[i],
-                                start=(c == 0 and i == 0),
-                                stop=(c == N_CHUNKS - 1 and i == SUB - 1),
-                            )
-                            nc.tensor.matmul(
-                                out=values[:, s, c * SUB + i, :], lhsT=blocks[i], rhs=ones[:, 0:2], start=True, stop=True
-                            )
+                        nc.tensor.transpose(
+                            bank[:, i, :], nat_words[:, i, 2 * g * P + u : 2 * (g + 1) * P : 2], ident_f32[:]
+                        )
+                    nc.scalar.copy(out=ag_words[c][:, a, :], in_=bank[:].rearrange("p i q -> p (i q)"))
+                    if g == 0:
+                        for e in range(2):
+                            j = 2 * a + e
+                            nc.vector.bn_stats(out=stats[:, j, c, :], in_=ag_values(c, j))
+                    q = a
+                    for i in range(SUB):
+                        block = ag_nat[:, i, K_PASS + q * P : K_PASS + (q + 1) * P]
+                        nc.tensor.matmul(
+                            out=squares[q][:],
+                            lhsT=block,
+                            rhs=block,
+                            start=(c == 0 and i == 0),
+                            stop=(c == N_CHUNKS - 1 and i == SUB - 1),
+                        )
+                        nc.tensor.matmul(
+                            out=values[:, q, c * SUB + i, :], lhsT=block, rhs=ones[:, 0:2], start=True, stop=True
+                        )
                 load_next_chunk()
+                if c == 0:
+                    load_weight(W_ag)
+                    group_weight(1)
 
-            vector_cols = turned.tile([P, PACK, P], BF16, tag="bank")
+            vector_cols = turned.tile([P, 2, PACK, P], BF16, tag="bank")
             for t in range(PACK):
-                nc.tensor.transpose(vector_cols[:, t, :], vector_rows[:, t::PACK], ident_bf16[:])
-            nc.scalar.copy(
-                out=gain_shift[:].rearrange("p (r t) -> p r t", t=PACK),
-                in_=vector_cols[:, :, 0 : 2 * PASSES].rearrange("p t r -> p r t"),
-            )
+                nc.tensor.transpose(vector_cols[:, 0, t, :], vector_rows[:, t::PACK], ident_bf16[:])
+                nc.tensor.transpose(vector_cols[:, 1, t, :], vector_rows[:, t * P : (t + 1) * P], ident_bf16[:])
+            for g in range(PASSES):
+                nc.scalar.copy(
+                    out=gain_shift[:, :, g * PACK : (g + 1) * PACK],
+                    in_=vector_cols[:, g, :, g : 2 * PASSES : PASSES].rearrange("p t v -> p v t"),
+                )
             bias_sum = turned.tile([P, COUT], F32, tag="bank")
             nc.tensor.matmul(out=bias_sum[:], lhsT=ones[:], rhs=bias_rows[:], start=True, stop=True)
             nc.scalar.copy(out=bias[:], in_=bias_sum[:])
@@ -286,16 +313,35 @@ def tile_geoconv_pb_t_kernel(tc, feat, ag, W_feat, b_feat, g1, be1, W_ag, b_ag, 
 
             nc.scalar.activation(out=std[:], in_=var, func=ACT.Sqrt, bias=eps[:], scale=1.0)
             nc.vector.reciprocal(out=inv_std[:], in_=std[:])
-            nc.vector.tensor_mul(out=bn_scale[:], in0=gain, in1=inv_std[:])
-            nc.vector.tensor_mul(out=scaled_mean[:], in0=mean, in1=bn_scale[:])
-            nc.vector.tensor_sub(out=bn_shift[:], in0=shift, in1=scaled_mean[:])
+            nc.vector.tensor_mul(out=scale_shift[:, 0, :], in0=gain, in1=inv_std[:])
+            nc.vector.tensor_mul(out=scaled_mean[:], in0=mean, in1=scale_shift[:, 0, :])
+            nc.vector.tensor_sub(out=scale_shift[:, 1, :], in0=shift, in1=scaled_mean[:])
 
             transpose_feat(1)
-            batch_norm(0)
+            batch_norm(0, 0)
+            relu_and_regroup(0, 0)
+            moved = turned.tile([P, PACK, 2, PACK], F32, tag="bank")
+            for t in range(PACK):
+                nc.tensor.matmul(
+                    out=moved[:, t, :, :],
+                    lhsT=select[:, t, :, :].rearrange("p q c -> p (q c)"),
+                    rhs=scale_shift[:, :, PACK:CH_TILES],
+                    start=True,
+                    stop=True,
+                )
+            nc.vector.tensor_tensor(
+                out=masked[:],
+                in0=moved[:].rearrange("p t v q -> p (t v) q"),
+                in1=quarter[:].unsqueeze(1).to_broadcast([P, PACK * 2, PACK]),
+                op=ALU.mult,
+            )
+            nc.vector.tensor_reduce(
+                out=scale_shift_1[:].rearrange("p t v -> p (t v)"), in_=masked[:], axis=AXIS.X, op=ALU.add
+            )
+            batch_norm(0, 1)
+            relu_and_regroup(0, 1)
             for g in range(PASSES):
-                relu_and_regroup(0, g, vector_regroups(0, g))
-            transpose_feat(2)
-            batch_norm(1)
+                batch_norm(1, g)
             for w in range(2):
                 nc.vector.quantize_mx(
                     out=w_codes[:, w, :, :].rearrange("p g n -> p (g n)").bitcast(FP8X4),
@@ -340,10 +386,11 @@ def tile_geoconv_pb_t_kernel(tc, feat, ag, W_feat, b_feat, g1, be1, W_ag, b_ag, 
                 transpose_feat(c + FEAT_TURN_AHEAD)
             multiply(c)
             if c + 2 < N_CHUNKS:
-                batch_norm(c + 2)
+                for g in range(PASSES):
+                    batch_norm(c + 2, g)
             if c + 1 < N_CHUNKS:
                 for g in range(PASSES):
-                    relu_and_regroup(c + 1, g, vector_regroups(c + 1, g))
+                    relu_and_regroup(c + 1, g)
                 quantise_feat(c + 1)
             add_bias_and_store(c, first_half)
         add_bias_and_store(N_CHUNKS - 1, second_half)

@@ -33,6 +33,8 @@ DVE_STAT_TILES = PACK
 PE_STAT_TILES = PACK
 TURN_BANKS = PSUM_BANKS - PE_STAT_TILES - 1
 PRODUCT_BANKS = PSUM_BANKS - TURN_BANKS
+SUM_COLUMNS = 16
+WARM_UP_MATMULS = 6
 FEAT_TURN_AHEAD = 2
 VECTOR_REGROUPS_EVERY = 4
 RUN = 4
@@ -72,7 +74,7 @@ def tile_geoconv_pb_t_kernel(tc, feat, ag, W_feat, b_feat, g1, be1, W_ag, b_ag, 
         table_warmer = keep.tile([P, 1], F32)
         nc.scalar.activation(out=table_warmer[:], in_=eps[:], func=ACT.Sqrt)
 
-        ones = keep.tile([P, P], BF16)
+        ones = keep.tile([P, COUT], BF16)
         nc.vector.memset(ones[:], 1.0)
         vector_rows = keep.tile([P, K_PASS], BF16)
         nc.vector.memset(vector_rows[:], 0.0)
@@ -139,7 +141,7 @@ def tile_geoconv_pb_t_kernel(tc, feat, ag, W_feat, b_feat, g1, be1, W_ag, b_ag, 
                 loaded.append(chunk)
 
         def load_weight(weight):
-            w_raw = natural.tile([P, PASSES, PACK * COUT], BF16, tag="natural", name="w_raw")
+            w_raw = feat_pool.tile([P, PASSES, PACK * COUT], BF16, align_bytes=64, tag="feat_grouped", name="w_raw")
             nc.sync.dma_start(out=w_raw[:], in_=weight.rearrange("(g p t) n -> p g (t n)", p=P, t=PACK))
             w_rows.append(w_raw[:].rearrange("p g (t n) -> p (g t) n", t=PACK))
 
@@ -150,26 +152,29 @@ def tile_geoconv_pb_t_kernel(tc, feat, ag, W_feat, b_feat, g1, be1, W_ag, b_ag, 
         h_operands = {}
         products = {}
 
-        def transpose_feat(c):
+        def transpose_feat(c, g):
             feat_words = loaded[N_CHUNKS + c][:].bitcast(F32)
-            feat_grouped[c] = feat_pool.tile([P, PASSES, CHUNK * PACK], BF16, align_bytes=64, name="feat_grouped")
+            if g == 0:
+                feat_grouped[c] = feat_pool.tile(
+                    [P, PASSES, CHUNK * PACK], BF16, align_bytes=64, tag="feat_grouped", name="grouped"
+                )
             grouped_words = feat_grouped[c][:].bitcast(F32)
-            for g in range(PASSES):
-                for i0 in range(0, SUB, 2):
-                    bank = turned.tile([P, 2, 2, P], F32, tag="bank")
-                    for u in range(2):
-                        for ii in range(2):
-                            first = 2 * g * P
-                            nc.tensor.transpose(
-                                bank[:, u, ii, :],
-                                feat_words[:, i0 + ii, first + u : first + 2 * P : 2],
-                                ident_f32[:],
-                            )
-                    nc.scalar.copy(
-                        out=grouped_words[:, g, i0 * P * 2 : (i0 + 2) * P * 2].rearrange("p (q u) -> p q u", u=2),
-                        in_=bank[:].rearrange("p u i q -> p (i q) u"),
-                    )
-            load_next_chunk()
+            for i0 in range(0, SUB, 2):
+                bank = turned.tile([P, 2, 2, P], F32, tag="bank")
+                for u in range(2):
+                    for ii in range(2):
+                        first = 2 * g * P
+                        nc.tensor.transpose(
+                            bank[:, u, ii, :],
+                            feat_words[:, i0 + ii, first + u : first + 2 * P : 2],
+                            ident_f32[:],
+                        )
+                nc.scalar.copy(
+                    out=grouped_words[:, g, i0 * P * 2 : (i0 + 2) * P * 2].rearrange("p (q u) -> p q u", u=2),
+                    in_=bank[:].rearrange("p u i q -> p (i q) u"),
+                )
+            if g == PASSES - 1:
+                load_next_chunk()
 
         def quantise_feat(c):
             feat_codes = feat_pool.tile([P, PASSES, CHUNK], U32, align_bytes=64)
@@ -219,12 +224,14 @@ def tile_geoconv_pb_t_kernel(tc, feat, ag, W_feat, b_feat, g1, be1, W_ag, b_ag, 
             w_stage = part1.enter_context(tc.tile_pool(name="w_stage", bufs=1))
             sums_psum = part1.enter_context(tc.psum_pool(name="sums_psum", bufs=1))
             squares = [sums_psum.tile([P, P], F32, name="squares%d" % s) for s in range(PE_STAT_TILES)]
-            values = sums_psum.tile([P, PE_STAT_TILES, N_CHUNKS * SUB, 2], F32)
+            values = sums_psum.tile([P, PE_STAT_TILES, 2 * N_CHUNKS * SUB + SUM_COLUMNS], F32)
 
             for k in range(NATURAL_BUFS - 2):
                 load_next_chunk()
             load_weight(W_feat)
-            load_next_chunk()
+            for k in range(2):
+                load_next_chunk()
+            load_weight(W_ag)
             w_grouped = w_stage.tile([P, 2, PASSES, COUT, PACK], BF16, align_bytes=64)
 
             def group_weight(w):
@@ -239,38 +246,49 @@ def tile_geoconv_pb_t_kernel(tc, feat, ag, W_feat, b_feat, g1, be1, W_ag, b_ag, 
                     )
 
             group_weight(0)
+            group_weight(1)
+
+            def keep_clock_up(count):
+                unread = turned.tile([P, COUT], F32, tag="bank", name="unread")
+                for k in range(count):
+                    nc.tensor.matmul(out=unread[:], lhsT=ones[:, 0:P], rhs=ones[:], start=True, stop=True)
+
+            keep_clock_up(WARM_UP_MATMULS)
             for c in range(N_CHUNKS):
                 ag_nat = loaded[c]
                 nat_words = ag_nat[:].bitcast(F32)
-                for a in range(2 * PASSES):
-                    g, u = divmod(a, 2)
-                    bank = turned.tile([P, SUB, P], F32, tag="bank")
-                    for i in range(SUB):
-                        nc.tensor.transpose(
-                            bank[:, i, :], nat_words[:, i, 2 * g * P + u : 2 * (g + 1) * P : 2], ident_f32[:]
-                        )
-                    nc.scalar.copy(out=ag_words[c][:, a, :], in_=bank[:].rearrange("p i q -> p (i q)"))
-                    if g == 0:
-                        for e in range(2):
-                            j = 2 * a + e
-                            nc.vector.bn_stats(out=stats[:, j, c, :], in_=ag_values(c, j))
-                    q = a
-                    for i in range(SUB):
-                        block = ag_nat[:, i, K_PASS + q * P : K_PASS + (q + 1) * P]
-                        nc.tensor.matmul(
-                            out=squares[q][:],
-                            lhsT=block,
-                            rhs=block,
-                            start=(c == 0 and i == 0),
-                            stop=(c == N_CHUNKS - 1 and i == SUB - 1),
-                        )
-                        nc.tensor.matmul(
-                            out=values[:, q, c * SUB + i, :], lhsT=block, rhs=ones[:, 0:2], start=True, stop=True
-                        )
+                for g in range(PASSES):
+                    for u in range(2):
+                        a = 2 * g + u
+                        bank = turned.tile([P, SUB, P], F32, tag="bank")
+                        for i in range(SUB):
+                            nc.tensor.transpose(
+                                bank[:, i, :], nat_words[:, i, 2 * g * P + u : 2 * (g + 1) * P : 2], ident_f32[:]
+                            )
+                        nc.scalar.copy(out=ag_words[c][:, a, :], in_=bank[:].rearrange("p i q -> p (i q)"))
+                        if g == 0:
+                            for e in range(2):
+                                j = 2 * a + e
+                                nc.vector.bn_stats(out=stats[:, j, c, :], in_=ag_values(c, j))
+                    for q in (2 * g, 2 * g + 1):
+                        for i in range(SUB):
+                            block = ag_nat[:, i, K_PASS + q * P : K_PASS + (q + 1) * P]
+                            nc.tensor.matmul(
+                                out=squares[q][:],
+                                lhsT=block,
+                                rhs=block,
+                                start=(c == 0 and i == 0),
+                                stop=(c == N_CHUNKS - 1 and i == SUB - 1),
+                            )
+                            b = c * SUB + i
+                            nc.tensor.matmul(
+                                out=values[:, q, 2 * b : 2 * b + SUM_COLUMNS],
+                                lhsT=block,
+                                rhs=ones[:, 0:SUM_COLUMNS],
+                                start=True,
+                                stop=True,
+                            )
                 load_next_chunk()
-                if c == 0:
-                    load_weight(W_ag)
-                    group_weight(1)
 
             vector_cols = turned.tile([P, 2, PACK, P], BF16, tag="bank")
             for t in range(PACK):
@@ -282,10 +300,13 @@ def tile_geoconv_pb_t_kernel(tc, feat, ag, W_feat, b_feat, g1, be1, W_ag, b_ag, 
                     in_=vector_cols[:, g, :, g : 2 * PASSES : PASSES].rearrange("p t v -> p v t"),
                 )
             bias_sum = turned.tile([P, COUT], F32, tag="bank")
-            nc.tensor.matmul(out=bias_sum[:], lhsT=ones[:], rhs=bias_rows[:], start=True, stop=True)
+            nc.tensor.matmul(out=bias_sum[:], lhsT=ones[:, 0:P], rhs=bias_rows[:], start=True, stop=True)
             nc.scalar.copy(out=bias[:], in_=bias_sum[:])
 
-            transpose_feat(0)
+            transpose_feat(0, 0)
+            keep_clock_up(2)
+            transpose_feat(0, 1)
+            keep_clock_up(2)
 
             for s in range(PE_STAT_TILES):
                 nc.vector.scalar_tensor_tensor(
@@ -297,7 +318,7 @@ def tile_geoconv_pb_t_kernel(tc, feat, ag, W_feat, b_feat, g1, be1, W_ag, b_ag, 
                     op1=ALU.mult,
                     accum_out=mean_of_squares[:, s : s + 1],
                 )
-            nc.vector.tensor_reduce(out=sum_of_values[:], in_=values[:, :, :, 0], axis=AXIS.X, op=ALU.add)
+            nc.vector.tensor_reduce(out=sum_of_values[:], in_=values[:, :, 0 : 2 * N_CHUNKS * SUB : 2], axis=AXIS.X, op=ALU.add)
             pe_mean = mean_var[:, DVE_STAT_TILES:CH_TILES, 0]
             pe_var = mean_var[:, DVE_STAT_TILES:CH_TILES, 1]
             chain = [
@@ -312,12 +333,20 @@ def tile_geoconv_pb_t_kernel(tc, feat, ag, W_feat, b_feat, g1, be1, W_ag, b_ag, 
                     chain[j]()
 
             nc.scalar.activation(out=std[:], in_=var, func=ACT.Sqrt, bias=eps[:], scale=1.0)
+            for w in range(2):
+                nc.vector.quantize_mx(
+                    out=w_codes[:, w, :, :].rearrange("p g n -> p (g n)").bitcast(FP8X4),
+                    scales=w_scales[:, w, :, :].rearrange("p g n -> p (g n)"),
+                    in_=w_grouped[:, w, :, :, :].rearrange("p g n t -> p (g n t)"),
+                )
             nc.vector.reciprocal(out=inv_std[:], in_=std[:])
             nc.vector.tensor_mul(out=scale_shift[:, 0, :], in0=gain, in1=inv_std[:])
             nc.vector.tensor_mul(out=scaled_mean[:], in0=mean, in1=scale_shift[:, 0, :])
             nc.vector.tensor_sub(out=scale_shift[:, 1, :], in0=shift, in1=scaled_mean[:])
 
-            transpose_feat(1)
+            transpose_feat(1, 0)
+            keep_clock_up(2)
+            transpose_feat(1, 1)
             batch_norm(0, 0)
             relu_and_regroup(0, 0)
             moved = turned.tile([P, PACK, 2, PACK], F32, tag="bank")
@@ -342,19 +371,13 @@ def tile_geoconv_pb_t_kernel(tc, feat, ag, W_feat, b_feat, g1, be1, W_ag, b_ag, 
             relu_and_regroup(0, 1)
             for g in range(PASSES):
                 batch_norm(1, g)
-            for w in range(2):
-                nc.vector.quantize_mx(
-                    out=w_codes[:, w, :, :].rearrange("p g n -> p (g n)").bitcast(FP8X4),
-                    scales=w_scales[:, w, :, :].rearrange("p g n -> p (g n)"),
-                    in_=w_grouped[:, w, :, :, :].rearrange("p g n t -> p (g n t)"),
-                )
             quantise_feat(0)
 
         result_pool = ctx.enter_context(tc.tile_pool(name="result_pool", bufs=8, reuse_waits="tile"))
         product_psum = ctx.enter_context(tc.psum_pool(name="product_psum", bufs=PRODUCT_BANKS, reuse_waits="tile"))
 
-        def multiply(c):
-            for i in range(SUB):
+        def multiply(c, sub_tiles):
+            for i in sub_tiles:
                 points = slice(i * P, (i + 1) * P)
                 product = product_psum.tile([P, COUT], F32, tag="bank", name="product")
                 for w, (codes, scales) in enumerate((feat_operands[c], h_operands[c])):
@@ -376,21 +399,21 @@ def tile_geoconv_pb_t_kernel(tc, feat, ag, W_feat, b_feat, g1, be1, W_ag, b_ag, 
                 nc.vector.tensor_tensor(out=result[:], in0=products[c, i][:], in1=bias[:], op=ALU.add)
                 nc.sync.dma_start(out=out_chunks[c][:, i, :], in_=result[:])
 
-        first_half = range(SUB // 2)
-        second_half = range(SUB // 2, SUB)
+        halves = (range(SUB // 2), range(SUB // 2, SUB))
         for c in range(N_CHUNKS):
             quantise_h(c)
             if c > 0:
-                add_bias_and_store(c - 1, second_half)
-            if c + FEAT_TURN_AHEAD < N_CHUNKS:
-                transpose_feat(c + FEAT_TURN_AHEAD)
-            multiply(c)
-            if c + 2 < N_CHUNKS:
-                for g in range(PASSES):
+                add_bias_and_store(c - 1, halves[1])
+            for g in range(PASSES):
+                if c + FEAT_TURN_AHEAD < N_CHUNKS:
+                    transpose_feat(c + FEAT_TURN_AHEAD, g)
+                multiply(c, halves[g])
+                if c + 2 < N_CHUNKS:
                     batch_norm(c + 2, g)
-            if c + 1 < N_CHUNKS:
-                for g in range(PASSES):
+                if c + 1 < N_CHUNKS:
                     relu_and_regroup(c + 1, g)
-                quantise_feat(c + 1)
-            add_bias_and_store(c, first_half)
-        add_bias_and_store(N_CHUNKS - 1, second_half)
+                if g == 0:
+                    add_bias_and_store(c, halves[0])
+                    if c + 1 < N_CHUNKS:
+                        quantise_feat(c + 1)
+        add_bias_and_store(N_CHUNKS - 1, halves[1])

@@ -25,17 +25,16 @@ SUB = 4
 CHUNK = P * SUB
 N_CHUNKS = POINTS // CHUNK
 PASSES = CHANNELS // K_PASS
-CH_TILES = CHANNELS // P
 BN_STATS_DIM = 6
 PSUM_BANKS = 8
 NATURAL_BUFS = 5
-DVE_STAT_TILES = PACK
 PE_STAT_TILES = PACK
+VECTOR_STAT_CHUNKS = (2, 5)
 TURN_BANKS = PSUM_BANKS - PE_STAT_TILES - 1
 PRODUCT_BANKS = PSUM_BANKS - TURN_BANKS
 SUM_COLUMNS = 16
 WARM_UP_MATMULS = 6
-FEAT_TURN_AHEAD = 2
+FEAT_TURN_AHEAD = 3
 VECTOR_REGROUPS_EVERY = 4
 RUN = 4
 
@@ -84,9 +83,7 @@ def tile_geoconv_pb_t_kernel(tc, feat, ag, W_feat, b_feat, g1, be1, W_ag, b_ag, 
         nc.vector.memset(bias_rows[:], 0.0)
         nc.scalar.dma_start(out=bias_rows[0:1, :], in_=b_feat.rearrange("(o n) -> o n", o=1))
         nc.scalar.dma_start(out=bias_rows[1:2, :], in_=b_ag.rearrange("(o n) -> o n", o=1))
-        gain_shift = keep.tile([P, 2, CH_TILES], F32)
-        gain = gain_shift[:, 0, :]
-        shift = gain_shift[:, 1, :]
+        gain_shift = keep.tile([P, 2, PASSES, PACK], F32)
         select = keep.tile([P, PACK, PACK, P // PACK], F32)
         for q in range(PACK):
             nc.gpsimd.tensor_scalar(
@@ -103,29 +100,36 @@ def tile_geoconv_pb_t_kernel(tc, feat, ag, W_feat, b_feat, g1, be1, W_ag, b_ag, 
         )
         bias = keep.tile([P, COUT], F32)
 
-        ag_words = [keep.tile([P, 2 * PASSES, CHUNK], F32, name="ag_words%d" % c) for c in range(N_CHUNKS)]
+        ag_words = [keep.tile([P, 2, CHUNK], F32, name="ag_words%d" % c) for c in range(N_CHUNKS)]
+        ag_rows = [keep.tile([P, PACK, CHUNK], BF16, name="ag_rows%d" % c) for c in range(N_CHUNKS)]
 
-        def ag_values(c, j):
-            return ag_words[c][:, j // 2, :].bitcast(BF16)[:, j % 2 :: 2]
+        def ag_values(c, g, t):
+            if g == 0:
+                return ag_words[c][:, t // 2, :].bitcast(BF16)[:, t % 2 :: 2]
+            return ag_rows[c][:, t, :]
 
         w_codes = keep.tile([P, 2, PASSES, COUT], U32, align_bytes=64)
         w_scales = keep.tile([P, 2, PASSES, COUT], U8, align_bytes=64)
-        stats = keep.tile([P, DVE_STAT_TILES, N_CHUNKS, BN_STATS_DIM], F32)
+        stats = [
+            keep.tile([P, PACK, N_CHUNKS, BN_STATS_DIM], F32, name="stats0"),
+            keep.tile([P, PACK, len(VECTOR_STAT_CHUNKS), BN_STATS_DIM], F32, name="stats1"),
+        ]
+        mean_var = [keep.tile([P, PACK, 2], F32, name="mean_var%d" % g) for g in range(PASSES)]
         diagonal = keep.tile([P, PE_STAT_TILES, P], F32)
-        mean_of_squares = keep.tile([P, PE_STAT_TILES], F32)
+        sums = keep.tile([P, 2, PE_STAT_TILES], F32)
         sum_of_values = keep.tile([P, PE_STAT_TILES], F32)
-        mean_squared = keep.tile([P, PE_STAT_TILES], F32)
-        mean_var = keep.tile([P, CH_TILES, 2], F32)
-        mean = mean_var[:, :, 0]
-        var = mean_var[:, :, 1]
-        std = keep.tile([P, CH_TILES], F32)
-        inv_std = keep.tile([P, CH_TILES], F32)
-        scale_shift = keep.tile([P, 2, CH_TILES], F32)
-        scaled_mean = keep.tile([P, CH_TILES], F32)
-        masked = keep.tile([P, PACK * 2, PACK], F32)
-        scale_shift_1 = keep.tile([P, PACK, 2], F32)
-        bn_scale = [scale_shift[:, 0, t : t + 1] for t in range(PACK)] + [scale_shift_1[:, t, 0:1] for t in range(PACK)]
-        bn_shift = [scale_shift[:, 1, t : t + 1] for t in range(PACK)] + [scale_shift_1[:, t, 1:2] for t in range(PACK)]
+        masked = keep.tile([P, 2 * PACK, PACK], F32)
+        moments = keep.tile([P, 2, PACK], F32)
+        vector_moments = keep.tile([P, 2, PACK], F32)
+        mean_squared = keep.tile([P, PACK], F32)
+        var_1 = keep.tile([P, PACK], F32)
+        mean = [mean_var[0][:, :, 0], moments[:, 1, :]]
+        var = [mean_var[0][:, :, 1], var_1[:]]
+        std = [keep.tile([P, PACK], F32, name="std%d" % g) for g in range(PASSES)]
+        inv_std = [keep.tile([P, PACK], F32, name="inv_std%d" % g) for g in range(PASSES)]
+        bn_scale = [keep.tile([P, PACK], F32, name="bn_scale%d" % g) for g in range(PASSES)]
+        scaled_mean = [keep.tile([P, PACK], F32, name="scaled_mean%d" % g) for g in range(PASSES)]
+        bn_shift = [keep.tile([P, PACK], F32, name="bn_shift%d" % g) for g in range(PASSES)]
 
         sources = [ag_chunks[c] for c in range(N_CHUNKS)] + [feat_chunks[c] for c in range(N_CHUNKS)]
         loaded = []
@@ -141,7 +145,7 @@ def tile_geoconv_pb_t_kernel(tc, feat, ag, W_feat, b_feat, g1, be1, W_ag, b_ag, 
                 loaded.append(chunk)
 
         def load_weight(weight):
-            w_raw = feat_pool.tile([P, PASSES, PACK * COUT], BF16, align_bytes=64, tag="feat_grouped", name="w_raw")
+            w_raw = feat_pool.tile([P, PASSES, PACK * COUT], BF16, align_bytes=64, bufs=4, tag="feat_grouped", name="w_raw")
             nc.sync.dma_start(out=w_raw[:], in_=weight.rearrange("(g p t) n -> p g (t n)", p=P, t=PACK))
             w_rows.append(w_raw[:].rearrange("p g (t n) -> p (g t) n", t=PACK))
 
@@ -156,7 +160,7 @@ def tile_geoconv_pb_t_kernel(tc, feat, ag, W_feat, b_feat, g1, be1, W_ag, b_ag, 
             feat_words = loaded[N_CHUNKS + c][:].bitcast(F32)
             if g == 0:
                 feat_grouped[c] = feat_pool.tile(
-                    [P, PASSES, CHUNK * PACK], BF16, align_bytes=64, tag="feat_grouped", name="grouped"
+                    [P, PASSES, CHUNK * PACK], BF16, align_bytes=64, bufs=4, tag="feat_grouped", name="grouped"
                 )
             grouped_words = feat_grouped[c][:].bitcast(F32)
             for i0 in range(0, SUB, 2):
@@ -189,12 +193,11 @@ def tile_geoconv_pb_t_kernel(tc, feat, ag, W_feat, b_feat, g1, be1, W_ag, b_ag, 
         def batch_norm(c, g):
             h_normed[c, g] = h_pool.tile([P, PACK, CHUNK], BF16, bufs=4, name="h_normed")
             for t in range(PACK):
-                j = g * PACK + t
                 nc.vector.tensor_scalar(
                     out=h_normed[c, g][:, t, :],
-                    in0=ag_values(c, j),
-                    scalar1=bn_scale[j],
-                    scalar2=bn_shift[j],
+                    in0=ag_values(c, g, t),
+                    scalar1=bn_scale[g][:, t : t + 1],
+                    scalar2=bn_shift[g][:, t : t + 1],
                     op0=ALU.mult,
                     op1=ALU.add,
                 )
@@ -224,7 +227,9 @@ def tile_geoconv_pb_t_kernel(tc, feat, ag, W_feat, b_feat, g1, be1, W_ag, b_ag, 
             w_stage = part1.enter_context(tc.tile_pool(name="w_stage", bufs=1))
             sums_psum = part1.enter_context(tc.psum_pool(name="sums_psum", bufs=1))
             squares = [sums_psum.tile([P, P], F32, name="squares%d" % s) for s in range(PE_STAT_TILES)]
-            values = sums_psum.tile([P, PE_STAT_TILES, 2 * N_CHUNKS * SUB + SUM_COLUMNS], F32)
+            pe_chunks = [c for c in range(N_CHUNKS) if c not in VECTOR_STAT_CHUNKS]
+            pe_blocks = len(pe_chunks) * SUB
+            values = sums_psum.tile([P, PE_STAT_TILES, 2 * pe_blocks + SUM_COLUMNS], F32)
 
             for k in range(NATURAL_BUFS - 2):
                 load_next_chunk()
@@ -234,19 +239,26 @@ def tile_geoconv_pb_t_kernel(tc, feat, ag, W_feat, b_feat, g1, be1, W_ag, b_ag, 
             load_weight(W_ag)
             w_grouped = w_stage.tile([P, 2, PASSES, COUT, PACK], BF16, align_bytes=64)
 
-            def group_weight(w):
-                for g in range(PASSES):
-                    nc.gpsimd.tensor_scalar(
-                        out=by_runs_dst(w_grouped[:, w, g, :, :]),
-                        in0=by_runs_src(w_rows[w][:, g * PACK : (g + 1) * PACK, :]),
-                        scalar1=1.0,
-                        scalar2=0.0,
-                        op0=ALU.mult,
-                        op1=ALU.add,
-                    )
+            def group_weight(w, g):
+                nc.gpsimd.tensor_scalar(
+                    out=by_runs_dst(w_grouped[:, w, g, :, :]),
+                    in0=by_runs_src(w_rows[w][:, g * PACK : (g + 1) * PACK, :]),
+                    scalar1=1.0,
+                    scalar2=0.0,
+                    op0=ALU.mult,
+                    op1=ALU.add,
+                )
 
-            group_weight(0)
-            group_weight(1)
+            def quantise_weight(w):
+                nc.vector.quantize_mx(
+                    out=w_codes[:, w, :, :].rearrange("p g n -> p (g n)").bitcast(FP8X4),
+                    scales=w_scales[:, w, :, :].rearrange("p g n -> p (g n)"),
+                    in_=w_grouped[:, w, :, :, :].rearrange("p g n t -> p (g n t)"),
+                )
+
+            for w in range(2):
+                for g in range(PASSES):
+                    group_weight(w, g)
 
             def keep_clock_up(count):
                 unread = turned.tile([P, COUT], F32, tag="bank", name="unread")
@@ -265,22 +277,27 @@ def tile_geoconv_pb_t_kernel(tc, feat, ag, W_feat, b_feat, g1, be1, W_ag, b_ag, 
                             nc.tensor.transpose(
                                 bank[:, i, :], nat_words[:, i, 2 * g * P + u : 2 * (g + 1) * P : 2], ident_f32[:]
                             )
-                        nc.scalar.copy(out=ag_words[c][:, a, :], in_=bank[:].rearrange("p i q -> p (i q)"))
+                        turned_words = bank[:].rearrange("p i q -> p (i q)")
                         if g == 0:
-                            for e in range(2):
-                                j = 2 * a + e
-                                nc.vector.bn_stats(out=stats[:, j, c, :], in_=ag_values(c, j))
+                            nc.scalar.copy(out=ag_words[c][:, u, :], in_=turned_words)
+                        else:
+                            nc.scalar.copy(
+                                out=ag_rows[c][:, 2 * u : 2 * u + 2, :],
+                                in_=turned_words.bitcast(BF16).rearrange("p (n e) -> p e n", e=2),
+                            )
+                        if g == 0 or c in VECTOR_STAT_CHUNKS:
+                            slot = c if g == 0 else VECTOR_STAT_CHUNKS.index(c)
+                            for t in (2 * u, 2 * u + 1):
+                                nc.vector.bn_stats(out=stats[g][:, t, slot, :], in_=ag_values(c, g, t))
+                    if c in VECTOR_STAT_CHUNKS:
+                        continue
                     for q in (2 * g, 2 * g + 1):
                         for i in range(SUB):
                             block = ag_nat[:, i, K_PASS + q * P : K_PASS + (q + 1) * P]
+                            b = pe_chunks.index(c) * SUB + i
                             nc.tensor.matmul(
-                                out=squares[q][:],
-                                lhsT=block,
-                                rhs=block,
-                                start=(c == 0 and i == 0),
-                                stop=(c == N_CHUNKS - 1 and i == SUB - 1),
+                                out=squares[q][:], lhsT=block, rhs=block, start=(b == 0), stop=(b == pe_blocks - 1)
                             )
-                            b = c * SUB + i
                             nc.tensor.matmul(
                                 out=values[:, q, 2 * b : 2 * b + SUM_COLUMNS],
                                 lhsT=block,
@@ -288,90 +305,99 @@ def tile_geoconv_pb_t_kernel(tc, feat, ag, W_feat, b_feat, g1, be1, W_ag, b_ag, 
                                 start=True,
                                 stop=True,
                             )
+                if c == VECTOR_STAT_CHUNKS[-1]:
+                    share = len(VECTOR_STAT_CHUNKS) / N_CHUNKS
+                    for t in range(PACK):
+                        nc.vector.bn_aggr(
+                            out=mean_var[1][:, t, :], in_=stats[1][:, t, :, :].rearrange("p c s -> p (c s)")
+                        )
+                    nc.vector.tensor_mul(out=mean_squared[:], in0=mean_var[1][:, :, 0], in1=mean_var[1][:, :, 0])
+                    nc.vector.tensor_add(out=var_1[:], in0=mean_squared[:], in1=mean_var[1][:, :, 1])
+                    nc.vector.tensor_scalar_mul(out=vector_moments[:, 0, :], in0=var_1[:], scalar1=share)
+                    nc.vector.tensor_scalar_mul(out=vector_moments[:, 1, :], in0=mean_var[1][:, :, 0], scalar1=share)
+                if c >= N_CHUNKS - 2:
+                    quantise_weight(c - N_CHUNKS + 2)
                 load_next_chunk()
 
-            vector_cols = turned.tile([P, 2, PACK, P], BF16, tag="bank")
+            vector_cols = turned.tile([P, PACK, P], BF16, tag="bank")
             for t in range(PACK):
-                nc.tensor.transpose(vector_cols[:, 0, t, :], vector_rows[:, t::PACK], ident_bf16[:])
-                nc.tensor.transpose(vector_cols[:, 1, t, :], vector_rows[:, t * P : (t + 1) * P], ident_bf16[:])
-            for g in range(PASSES):
-                nc.scalar.copy(
-                    out=gain_shift[:, :, g * PACK : (g + 1) * PACK],
-                    in_=vector_cols[:, g, :, g : 2 * PASSES : PASSES].rearrange("p t v -> p v t"),
-                )
+                nc.tensor.transpose(vector_cols[:, t, :], vector_rows[:, t::PACK], ident_bf16[:])
+            nc.scalar.copy(
+                out=gain_shift[:].rearrange("p v g t -> p (v g) t"),
+                in_=vector_cols[:, :, 0 : 2 * PASSES].rearrange("p t r -> p r t"),
+            )
             bias_sum = turned.tile([P, COUT], F32, tag="bank")
             nc.tensor.matmul(out=bias_sum[:], lhsT=ones[:, 0:P], rhs=bias_rows[:], start=True, stop=True)
             nc.scalar.copy(out=bias[:], in_=bias_sum[:])
 
+            def scale_and_shift(g):
+                nc.vector.reciprocal(out=inv_std[g][:], in_=std[g][:])
+                nc.vector.tensor_mul(out=bn_scale[g][:], in0=gain_shift[:, 0, g, :], in1=inv_std[g][:])
+                nc.vector.tensor_mul(out=scaled_mean[g][:], in0=mean[g], in1=bn_scale[g][:])
+                nc.vector.tensor_sub(out=bn_shift[g][:], in0=gain_shift[:, 1, g, :], in1=scaled_mean[g][:])
+
             transpose_feat(0, 0)
             keep_clock_up(2)
-            transpose_feat(0, 1)
-            keep_clock_up(2)
-
-            for s in range(PE_STAT_TILES):
+            for t in range(PACK):
+                nc.vector.bn_aggr(out=mean_var[0][:, t, :], in_=stats[0][:, t, :, :].rearrange("p c s -> p (c s)"))
+            nc.scalar.activation(out=std[0][:], in_=var[0], func=ACT.Sqrt, bias=eps[:], scale=1.0)
+            for q in range(PE_STAT_TILES):
                 nc.vector.scalar_tensor_tensor(
-                    out=diagonal[:, s, :],
-                    in0=squares[s][:],
+                    out=diagonal[:, q, :],
+                    in0=squares[q][:],
                     scalar=1.0 / POINTS,
                     in1=ident_f32[:],
                     op0=ALU.mult,
                     op1=ALU.mult,
-                    accum_out=mean_of_squares[:, s : s + 1],
+                    accum_out=sums[:, 0, q : q + 1],
                 )
-            nc.vector.tensor_reduce(out=sum_of_values[:], in_=values[:, :, 0 : 2 * N_CHUNKS * SUB : 2], axis=AXIS.X, op=ALU.add)
-            pe_mean = mean_var[:, DVE_STAT_TILES:CH_TILES, 0]
-            pe_var = mean_var[:, DVE_STAT_TILES:CH_TILES, 1]
-            chain = [
-                lambda: nc.vector.tensor_scalar_mul(out=pe_mean, in0=sum_of_values[:], scalar1=1.0 / POINTS),
-                lambda: nc.vector.tensor_mul(out=mean_squared[:], in0=pe_mean, in1=pe_mean),
-                lambda: nc.vector.tensor_sub(out=pe_var, in0=mean_of_squares[:], in1=mean_squared[:]),
-                lambda: nc.vector.tensor_scalar_max(out=pe_var, in0=pe_var, scalar1=0.0),
-            ]
-            for j in range(DVE_STAT_TILES):
-                nc.vector.bn_aggr(out=mean_var[:, j, :], in_=stats[:, j, :, :].rearrange("p c s -> p (c s)"))
-                if j < len(chain):
-                    chain[j]()
-
-            nc.scalar.activation(out=std[:], in_=var, func=ACT.Sqrt, bias=eps[:], scale=1.0)
-            for w in range(2):
-                nc.vector.quantize_mx(
-                    out=w_codes[:, w, :, :].rearrange("p g n -> p (g n)").bitcast(FP8X4),
-                    scales=w_scales[:, w, :, :].rearrange("p g n -> p (g n)"),
-                    in_=w_grouped[:, w, :, :, :].rearrange("p g n t -> p (g n t)"),
-                )
-            nc.vector.reciprocal(out=inv_std[:], in_=std[:])
-            nc.vector.tensor_mul(out=scale_shift[:, 0, :], in0=gain, in1=inv_std[:])
-            nc.vector.tensor_mul(out=scaled_mean[:], in0=mean, in1=scale_shift[:, 0, :])
-            nc.vector.tensor_sub(out=scale_shift[:, 1, :], in0=shift, in1=scaled_mean[:])
-
-            transpose_feat(1, 0)
-            keep_clock_up(2)
-            transpose_feat(1, 1)
+            nc.vector.tensor_reduce(
+                out=sum_of_values[:], in_=values[:, :, 0 : 2 * pe_blocks : 2], axis=AXIS.X, op=ALU.add
+            )
+            nc.vector.tensor_scalar_mul(out=sums[:, 1, :], in0=sum_of_values[:], scalar1=1.0 / POINTS)
+            transpose_feat(0, 1)
+            scale_and_shift(0)
             batch_norm(0, 0)
-            relu_and_regroup(0, 0)
             moved = turned.tile([P, PACK, 2, PACK], F32, tag="bank")
             for t in range(PACK):
                 nc.tensor.matmul(
-                    out=moved[:, t, :, :],
+                    out=moved[:, t, :, :].rearrange("p v q -> p (v q)"),
                     lhsT=select[:, t, :, :].rearrange("p q c -> p (q c)"),
-                    rhs=scale_shift[:, :, PACK:CH_TILES],
+                    rhs=sums[:].rearrange("p v q -> p (v q)"),
                     start=True,
                     stop=True,
                 )
+            keep_clock_up(2)
             nc.vector.tensor_tensor(
                 out=masked[:],
                 in0=moved[:].rearrange("p t v q -> p (t v) q"),
-                in1=quarter[:].unsqueeze(1).to_broadcast([P, PACK * 2, PACK]),
+                in1=quarter[:].unsqueeze(1).to_broadcast([P, 2 * PACK, PACK]),
                 op=ALU.mult,
             )
             nc.vector.tensor_reduce(
-                out=scale_shift_1[:].rearrange("p t v -> p (t v)"), in_=masked[:], axis=AXIS.X, op=ALU.add
+                out=moments[:].rearrange("p v t -> p t v"),
+                in_=masked[:].rearrange("p (t v) q -> p t v q", v=2),
+                axis=AXIS.X,
+                op=ALU.add,
             )
+            nc.vector.tensor_add(out=moments[:], in0=moments[:], in1=vector_moments[:])
+            nc.vector.tensor_mul(out=mean_squared[:], in0=mean[1], in1=mean[1])
+            nc.vector.tensor_sub(out=var_1[:], in0=moments[:, 0, :], in1=mean_squared[:])
+            nc.vector.tensor_scalar_max(out=var_1[:], in0=var_1[:], scalar1=0.0)
+            transpose_feat(1, 0)
+            nc.scalar.activation(out=std[1][:], in_=var[1], func=ACT.Sqrt, bias=eps[:], scale=1.0)
+            relu_and_regroup(0, 0)
+            transpose_feat(1, 1)
+            keep_clock_up(2)
+            quantise_feat(0)
+            scale_and_shift(1)
             batch_norm(0, 1)
             relu_and_regroup(0, 1)
             for g in range(PASSES):
+                transpose_feat(2, g)
+            quantise_h(0)
+            for g in range(PASSES):
                 batch_norm(1, g)
-            quantise_feat(0)
 
         result_pool = ctx.enter_context(tc.tile_pool(name="result_pool", bufs=8, reuse_waits="tile"))
         product_psum = ctx.enter_context(tc.psum_pool(name="product_psum", bufs=PRODUCT_BANKS, reuse_waits="tile"))
@@ -401,8 +427,8 @@ def tile_geoconv_pb_t_kernel(tc, feat, ag, W_feat, b_feat, g1, be1, W_ag, b_ag, 
 
         halves = (range(SUB // 2), range(SUB // 2, SUB))
         for c in range(N_CHUNKS):
-            quantise_h(c)
             if c > 0:
+                quantise_h(c)
                 add_bias_and_store(c - 1, halves[1])
             for g in range(PASSES):
                 if c + FEAT_TURN_AHEAD < N_CHUNKS:

@@ -29,9 +29,12 @@ BN_STATS_DIM = 6
 PSUM_BANKS = 8
 NATURAL_BUFS = 5
 PE_STAT_TILES = PACK
-VECTOR_STAT_CHUNKS = (2, 5)
-TURN_BANKS = PSUM_BANKS - PE_STAT_TILES - 1
-PRODUCT_BANKS = PSUM_BANKS - TURN_BANKS
+VECTOR_SUB_TILE = SUB - 1
+VECTOR_SUB_TILE_CHUNKS = 4
+AG_TURN_BANKS = PSUM_BANKS - PE_STAT_TILES - 1
+FEAT_TURN_BANKS = SUB
+PRODUCT_BANKS = PSUM_BANKS - FEAT_TURN_BANKS
+WEIGHT_CHUNKS = (5, 6)
 SUM_COLUMNS = 16
 WARM_UP_MATMULS = 6
 FEAT_TURN_AHEAD = 3
@@ -61,17 +64,16 @@ def tile_geoconv_pb_t_kernel(tc, feat, ag, W_feat, b_feat, g1, be1, W_ag, b_ag, 
         feat_pool = ctx.enter_context(tc.tile_pool(name="feat_pool", bufs=3))
         h_pool = ctx.enter_context(tc.tile_pool(name="h_pool", bufs=2))
         natural = ctx.enter_context(tc.tile_pool(name="natural", bufs=NATURAL_BUFS, side="right"))
-        turned = ctx.enter_context(tc.psum_pool(name="turned", bufs=TURN_BANKS))
 
         ident_bf16 = keep.tile([P, P], BF16)
         make_identity(nc, ident_bf16[:])
         ident_f32 = keep.tile([P, P], F32)
         make_identity(nc, ident_f32[:])
 
-        eps = keep.tile([P, 1], F32)
-        nc.vector.memset(eps[:], BN_EPS)
-        table_warmer = keep.tile([P, 1], F32)
-        nc.scalar.activation(out=table_warmer[:], in_=eps[:], func=ACT.Sqrt)
+        minus_half = keep.tile([P, PACK], F32)
+        nc.vector.memset(minus_half[:], -0.5)
+        table_warmer = keep.tile([P, PACK], F32)
+        nc.scalar.activation(out=table_warmer[:], in_=minus_half[:], func=ACT.Relu)
 
         ones = keep.tile([P, COUT], BF16)
         nc.vector.memset(ones[:], 1.0)
@@ -100,19 +102,13 @@ def tile_geoconv_pb_t_kernel(tc, feat, ag, W_feat, b_feat, g1, be1, W_ag, b_ag, 
         )
         bias = keep.tile([P, COUT], F32)
 
-        ag_words = [keep.tile([P, 2, CHUNK], F32, name="ag_words%d" % c) for c in range(N_CHUNKS)]
-        ag_rows = [keep.tile([P, PACK, CHUNK], BF16, name="ag_rows%d" % c) for c in range(N_CHUNKS)]
-
-        def ag_values(c, g, t):
-            if g == 0:
-                return ag_words[c][:, t // 2, :].bitcast(BF16)[:, t % 2 :: 2]
-            return ag_rows[c][:, t, :]
+        ag_t = [keep.tile([P, PASSES * PACK, CHUNK], BF16, name="ag_t%d" % c) for c in range(N_CHUNKS)]
 
         w_codes = keep.tile([P, 2, PASSES, COUT], U32, align_bytes=64)
         w_scales = keep.tile([P, 2, PASSES, COUT], U8, align_bytes=64)
         stats = [
             keep.tile([P, PACK, N_CHUNKS, BN_STATS_DIM], F32, name="stats0"),
-            keep.tile([P, PACK, len(VECTOR_STAT_CHUNKS), BN_STATS_DIM], F32, name="stats1"),
+            keep.tile([P, PACK, VECTOR_SUB_TILE_CHUNKS, BN_STATS_DIM], F32, name="stats1"),
         ]
         mean_var = [keep.tile([P, PACK, 2], F32, name="mean_var%d" % g) for g in range(PASSES)]
         diagonal = keep.tile([P, PE_STAT_TILES, P], F32)
@@ -124,8 +120,7 @@ def tile_geoconv_pb_t_kernel(tc, feat, ag, W_feat, b_feat, g1, be1, W_ag, b_ag, 
         mean_squared = keep.tile([P, PACK], F32)
         var_1 = keep.tile([P, PACK], F32)
         mean = [mean_var[0][:, :, 0], moments[:, 1, :]]
-        var = [mean_var[0][:, :, 1], var_1[:]]
-        std = [keep.tile([P, PACK], F32, name="std%d" % g) for g in range(PASSES)]
+        var_eps = [keep.tile([P, PACK], F32, name="var_eps%d" % g) for g in range(PASSES)]
         inv_std = [keep.tile([P, PACK], F32, name="inv_std%d" % g) for g in range(PASSES)]
         bn_scale = [keep.tile([P, PACK], F32, name="bn_scale%d" % g) for g in range(PASSES)]
         scaled_mean = [keep.tile([P, PACK], F32, name="scaled_mean%d" % g) for g in range(PASSES)]
@@ -156,29 +151,33 @@ def tile_geoconv_pb_t_kernel(tc, feat, ag, W_feat, b_feat, g1, be1, W_ag, b_ag, 
         h_operands = {}
         products = {}
 
-        def transpose_feat(c, g):
+        def keep_clock_up(pool, count):
+            unread = pool.tile([P, COUT], F32, tag="bank", name="unread")
+            for k in range(count):
+                nc.tensor.matmul(out=unread[:], lhsT=ones[:, 0:P], rhs=ones[:], start=True, stop=True)
+
+        def transpose_feat(c):
             feat_words = loaded[N_CHUNKS + c][:].bitcast(F32)
-            if g == 0:
-                feat_grouped[c] = feat_pool.tile(
-                    [P, PASSES, CHUNK * PACK], BF16, align_bytes=64, bufs=4, tag="feat_grouped", name="grouped"
-                )
+            feat_grouped[c] = feat_pool.tile(
+                [P, PASSES, CHUNK * PACK], BF16, align_bytes=64, bufs=4, tag="feat_grouped", name="grouped"
+            )
             grouped_words = feat_grouped[c][:].bitcast(F32)
-            for i0 in range(0, SUB, 2):
-                bank = turned.tile([P, 2, 2, P], F32, tag="bank")
-                for u in range(2):
-                    for ii in range(2):
-                        first = 2 * g * P
-                        nc.tensor.transpose(
-                            bank[:, u, ii, :],
-                            feat_words[:, i0 + ii, first + u : first + 2 * P : 2],
-                            ident_f32[:],
-                        )
-                nc.scalar.copy(
-                    out=grouped_words[:, g, i0 * P * 2 : (i0 + 2) * P * 2].rearrange("p (q u) -> p q u", u=2),
-                    in_=bank[:].rearrange("p u i q -> p (i q) u"),
-                )
-            if g == PASSES - 1:
-                load_next_chunk()
+            for g in range(PASSES):
+                for i0 in range(0, SUB, 2):
+                    bank = turned.tile([P, 2, 2, P], F32, tag="bank")
+                    for u in range(2):
+                        for ii in range(2):
+                            first = 2 * g * P
+                            nc.tensor.transpose(
+                                bank[:, u, ii, :],
+                                feat_words[:, i0 + ii, first + u : first + 2 * P : 2],
+                                ident_f32[:],
+                            )
+                    nc.scalar.copy(
+                        out=grouped_words[:, g, i0 * P * 2 : (i0 + 2) * P * 2].rearrange("p (q u) -> p q u", u=2),
+                        in_=bank[:].rearrange("p u i q -> p (i q) u"),
+                    )
+            load_next_chunk()
 
         def quantise_feat(c):
             feat_codes = feat_pool.tile([P, PASSES, CHUNK], U32, align_bytes=64)
@@ -190,12 +189,20 @@ def tile_geoconv_pb_t_kernel(tc, feat, ag, W_feat, b_feat, g1, be1, W_ag, b_ag, 
             )
             feat_operands[c] = (feat_codes, feat_scales)
 
+        def one_over_root(g):
+            nc.gpsimd.tensor_tensor(out=inv_std[g][:], in0=var_eps[g][:], in1=minus_half[:], op=ALU.pow)
+
+        def scale_and_shift(g):
+            nc.vector.tensor_mul(out=bn_scale[g][:], in0=gain_shift[:, 0, g, :], in1=inv_std[g][:])
+            nc.vector.tensor_mul(out=scaled_mean[g][:], in0=mean[g], in1=bn_scale[g][:])
+            nc.vector.tensor_sub(out=bn_shift[g][:], in0=gain_shift[:, 1, g, :], in1=scaled_mean[g][:])
+
         def batch_norm(c, g):
             h_normed[c, g] = h_pool.tile([P, PACK, CHUNK], BF16, bufs=4, name="h_normed")
             for t in range(PACK):
                 nc.vector.tensor_scalar(
                     out=h_normed[c, g][:, t, :],
-                    in0=ag_values(c, g, t),
+                    in0=ag_t[c][:, g * PACK + t, :],
                     scalar1=bn_scale[g][:, t : t + 1],
                     scalar2=bn_shift[g][:, t : t + 1],
                     op0=ALU.mult,
@@ -227,8 +234,14 @@ def tile_geoconv_pb_t_kernel(tc, feat, ag, W_feat, b_feat, g1, be1, W_ag, b_ag, 
             w_stage = part1.enter_context(tc.tile_pool(name="w_stage", bufs=1))
             sums_psum = part1.enter_context(tc.psum_pool(name="sums_psum", bufs=1))
             squares = [sums_psum.tile([P, P], F32, name="squares%d" % s) for s in range(PE_STAT_TILES)]
-            pe_chunks = [c for c in range(N_CHUNKS) if c not in VECTOR_STAT_CHUNKS]
-            pe_blocks = len(pe_chunks) * SUB
+            pe_order = [
+                (c, i)
+                for c in range(N_CHUNKS)
+                for i in range(SUB)
+                if c >= VECTOR_SUB_TILE_CHUNKS or i != VECTOR_SUB_TILE
+            ]
+            pe_blocks = len(pe_order)
+            turned = part1.enter_context(tc.psum_pool(name="turned", bufs=AG_TURN_BANKS))
             values = sums_psum.tile([P, PE_STAT_TILES, 2 * pe_blocks + SUM_COLUMNS], F32)
 
             for k in range(NATURAL_BUFS - 2):
@@ -260,53 +273,41 @@ def tile_geoconv_pb_t_kernel(tc, feat, ag, W_feat, b_feat, g1, be1, W_ag, b_ag, 
                 for g in range(PASSES):
                     group_weight(w, g)
 
-            def keep_clock_up(count):
-                unread = turned.tile([P, COUT], F32, tag="bank", name="unread")
-                for k in range(count):
-                    nc.tensor.matmul(out=unread[:], lhsT=ones[:, 0:P], rhs=ones[:], start=True, stop=True)
-
-            keep_clock_up(WARM_UP_MATMULS)
+            keep_clock_up(turned, WARM_UP_MATMULS)
             for c in range(N_CHUNKS):
                 ag_nat = loaded[c]
-                nat_words = ag_nat[:].bitcast(F32)
-                for g in range(PASSES):
-                    for u in range(2):
-                        a = 2 * g + u
-                        bank = turned.tile([P, SUB, P], F32, tag="bank")
+                for q in range(PACK):
+                    for j in (2 * q, 2 * q + 1):
+                        g, t = divmod(j, PACK)
+                        bank = turned.tile([P, SUB, P], BF16, tag="bank")
                         for i in range(SUB):
-                            nc.tensor.transpose(
-                                bank[:, i, :], nat_words[:, i, 2 * g * P + u : 2 * (g + 1) * P : 2], ident_f32[:]
-                            )
-                        turned_words = bank[:].rearrange("p i q -> p (i q)")
+                            every_4th = ag_nat[:, i, g * K_PASS + t : (g + 1) * K_PASS : PACK]
+                            nc.tensor.transpose(bank[:, i, :], every_4th, ident_bf16[:])
+                        nc.scalar.copy(
+                            out=ag_t[c][:, j, :].bitcast(F32), in_=bank[:].rearrange("p i q -> p (i q)").bitcast(F32)
+                        )
                         if g == 0:
-                            nc.scalar.copy(out=ag_words[c][:, u, :], in_=turned_words)
-                        else:
-                            nc.scalar.copy(
-                                out=ag_rows[c][:, 2 * u : 2 * u + 2, :],
-                                in_=turned_words.bitcast(BF16).rearrange("p (n e) -> p e n", e=2),
-                            )
-                        if g == 0 or c in VECTOR_STAT_CHUNKS:
-                            slot = c if g == 0 else VECTOR_STAT_CHUNKS.index(c)
-                            for t in (2 * u, 2 * u + 1):
-                                nc.vector.bn_stats(out=stats[g][:, t, slot, :], in_=ag_values(c, g, t))
-                    if c in VECTOR_STAT_CHUNKS:
-                        continue
-                    for q in (2 * g, 2 * g + 1):
-                        for i in range(SUB):
-                            block = ag_nat[:, i, K_PASS + q * P : K_PASS + (q + 1) * P]
-                            b = pe_chunks.index(c) * SUB + i
-                            nc.tensor.matmul(
-                                out=squares[q][:], lhsT=block, rhs=block, start=(b == 0), stop=(b == pe_blocks - 1)
-                            )
-                            nc.tensor.matmul(
-                                out=values[:, q, 2 * b : 2 * b + SUM_COLUMNS],
-                                lhsT=block,
-                                rhs=ones[:, 0:SUM_COLUMNS],
-                                start=True,
-                                stop=True,
-                            )
-                if c == VECTOR_STAT_CHUNKS[-1]:
-                    share = len(VECTOR_STAT_CHUNKS) / N_CHUNKS
+                            nc.vector.bn_stats(out=stats[0][:, t, c, :], in_=ag_t[c][:, j, :])
+                        elif c < VECTOR_SUB_TILE_CHUNKS:
+                            sub_tile = slice(VECTOR_SUB_TILE * P, (VECTOR_SUB_TILE + 1) * P)
+                            nc.vector.bn_stats(out=stats[1][:, t, c, :], in_=ag_t[c][:, j, sub_tile])
+                    for i in range(SUB):
+                        if (c, i) not in pe_order:
+                            continue
+                        block = ag_nat[:, i, K_PASS + q * P : K_PASS + (q + 1) * P]
+                        b = pe_order.index((c, i))
+                        nc.tensor.matmul(
+                            out=squares[q][:], lhsT=block, rhs=block, start=(b == 0), stop=(b == pe_blocks - 1)
+                        )
+                        nc.tensor.matmul(
+                            out=values[:, q, 2 * b : 2 * b + SUM_COLUMNS],
+                            lhsT=block,
+                            rhs=ones[:, 0:SUM_COLUMNS],
+                            start=True,
+                            stop=True,
+                        )
+                if c == VECTOR_SUB_TILE_CHUNKS:
+                    share = VECTOR_SUB_TILE_CHUNKS * P / POINTS
                     for t in range(PACK):
                         nc.vector.bn_aggr(
                             out=mean_var[1][:, t, :], in_=stats[1][:, t, :, :].rearrange("p c s -> p (c s)")
@@ -315,8 +316,8 @@ def tile_geoconv_pb_t_kernel(tc, feat, ag, W_feat, b_feat, g1, be1, W_ag, b_ag, 
                     nc.vector.tensor_add(out=var_1[:], in0=mean_squared[:], in1=mean_var[1][:, :, 1])
                     nc.vector.tensor_scalar_mul(out=vector_moments[:, 0, :], in0=var_1[:], scalar1=share)
                     nc.vector.tensor_scalar_mul(out=vector_moments[:, 1, :], in0=mean_var[1][:, :, 0], scalar1=share)
-                if c >= N_CHUNKS - 2:
-                    quantise_weight(c - N_CHUNKS + 2)
+                if c in WEIGHT_CHUNKS:
+                    quantise_weight(WEIGHT_CHUNKS.index(c))
                 load_next_chunk()
 
             vector_cols = turned.tile([P, PACK, P], BF16, tag="bank")
@@ -330,17 +331,10 @@ def tile_geoconv_pb_t_kernel(tc, feat, ag, W_feat, b_feat, g1, be1, W_ag, b_ag, 
             nc.tensor.matmul(out=bias_sum[:], lhsT=ones[:, 0:P], rhs=bias_rows[:], start=True, stop=True)
             nc.scalar.copy(out=bias[:], in_=bias_sum[:])
 
-            def scale_and_shift(g):
-                nc.vector.reciprocal(out=inv_std[g][:], in_=std[g][:])
-                nc.vector.tensor_mul(out=bn_scale[g][:], in0=gain_shift[:, 0, g, :], in1=inv_std[g][:])
-                nc.vector.tensor_mul(out=scaled_mean[g][:], in0=mean[g], in1=bn_scale[g][:])
-                nc.vector.tensor_sub(out=bn_shift[g][:], in0=gain_shift[:, 1, g, :], in1=scaled_mean[g][:])
-
-            transpose_feat(0, 0)
-            keep_clock_up(2)
             for t in range(PACK):
                 nc.vector.bn_aggr(out=mean_var[0][:, t, :], in_=stats[0][:, t, :, :].rearrange("p c s -> p (c s)"))
-            nc.scalar.activation(out=std[0][:], in_=var[0], func=ACT.Sqrt, bias=eps[:], scale=1.0)
+            nc.vector.tensor_scalar_add(out=var_eps[0][:], in0=mean_var[0][:, :, 1], scalar1=BN_EPS)
+            one_over_root(0)
             for q in range(PE_STAT_TILES):
                 nc.vector.scalar_tensor_tensor(
                     out=diagonal[:, q, :],
@@ -355,55 +349,57 @@ def tile_geoconv_pb_t_kernel(tc, feat, ag, W_feat, b_feat, g1, be1, W_ag, b_ag, 
                 out=sum_of_values[:], in_=values[:, :, 0 : 2 * pe_blocks : 2], axis=AXIS.X, op=ALU.add
             )
             nc.vector.tensor_scalar_mul(out=sums[:, 1, :], in0=sum_of_values[:], scalar1=1.0 / POINTS)
-            transpose_feat(0, 1)
-            scale_and_shift(0)
-            batch_norm(0, 0)
-            moved = turned.tile([P, PACK, 2, PACK], F32, tag="bank")
-            for t in range(PACK):
-                nc.tensor.matmul(
-                    out=moved[:, t, :, :].rearrange("p v q -> p (v q)"),
-                    lhsT=select[:, t, :, :].rearrange("p q c -> p (q c)"),
-                    rhs=sums[:].rearrange("p v q -> p (v q)"),
-                    start=True,
-                    stop=True,
-                )
-            keep_clock_up(2)
-            nc.vector.tensor_tensor(
-                out=masked[:],
-                in0=moved[:].rearrange("p t v q -> p (t v) q"),
-                in1=quarter[:].unsqueeze(1).to_broadcast([P, 2 * PACK, PACK]),
-                op=ALU.mult,
-            )
-            nc.vector.tensor_reduce(
-                out=moments[:].rearrange("p v t -> p t v"),
-                in_=masked[:].rearrange("p (t v) q -> p t v q", v=2),
-                axis=AXIS.X,
-                op=ALU.add,
-            )
-            nc.vector.tensor_add(out=moments[:], in0=moments[:], in1=vector_moments[:])
-            nc.vector.tensor_mul(out=mean_squared[:], in0=mean[1], in1=mean[1])
-            nc.vector.tensor_sub(out=var_1[:], in0=moments[:, 0, :], in1=mean_squared[:])
-            nc.vector.tensor_scalar_max(out=var_1[:], in0=var_1[:], scalar1=0.0)
-            transpose_feat(1, 0)
-            nc.scalar.activation(out=std[1][:], in_=var[1], func=ACT.Sqrt, bias=eps[:], scale=1.0)
-            relu_and_regroup(0, 0)
-            transpose_feat(1, 1)
-            keep_clock_up(2)
-            quantise_feat(0)
-            scale_and_shift(1)
-            batch_norm(0, 1)
-            relu_and_regroup(0, 1)
-            for g in range(PASSES):
-                transpose_feat(2, g)
-            quantise_h(0)
-            for g in range(PASSES):
-                batch_norm(1, g)
 
         result_pool = ctx.enter_context(tc.tile_pool(name="result_pool", bufs=8, reuse_waits="tile"))
+        turned = ctx.enter_context(tc.psum_pool(name="feat_turned", bufs=FEAT_TURN_BANKS, reuse_waits="tile"))
         product_psum = ctx.enter_context(tc.psum_pool(name="product_psum", bufs=PRODUCT_BANKS, reuse_waits="tile"))
 
-        def multiply(c, sub_tiles):
-            for i in sub_tiles:
+        transpose_feat(0)
+        keep_clock_up(product_psum, 2)
+        transpose_feat(1)
+        scale_and_shift(0)
+        batch_norm(0, 0)
+        relu_and_regroup(0, 0)
+        moved = product_psum.tile([P, PACK, 2, PACK], F32, tag="bank")
+        for t in range(PACK):
+            nc.tensor.matmul(
+                out=moved[:, t, :, :].rearrange("p v q -> p (v q)"),
+                lhsT=select[:, t, :, :].rearrange("p q c -> p (q c)"),
+                rhs=sums[:].rearrange("p v q -> p (v q)"),
+                start=True,
+                stop=True,
+            )
+        keep_clock_up(product_psum, 2)
+        nc.vector.tensor_tensor(
+            out=masked[:],
+            in0=moved[:].rearrange("p t v q -> p (t v) q"),
+            in1=quarter[:].unsqueeze(1).to_broadcast([P, 2 * PACK, PACK]),
+            op=ALU.mult,
+        )
+        nc.vector.tensor_reduce(
+            out=moments[:].rearrange("p v t -> p t v"),
+            in_=masked[:].rearrange("p (t v) q -> p t v q", v=2),
+            axis=AXIS.X,
+            op=ALU.add,
+        )
+        nc.vector.tensor_add(out=moments[:], in0=moments[:], in1=vector_moments[:])
+        nc.vector.tensor_mul(out=mean_squared[:], in0=mean[1], in1=mean[1])
+        nc.vector.tensor_sub(out=var_1[:], in0=moments[:, 0, :], in1=mean_squared[:])
+        nc.vector.tensor_scalar(
+            out=var_eps[1][:], in0=var_1[:], scalar1=0.0, scalar2=BN_EPS, op0=ALU.max, op1=ALU.add
+        )
+        one_over_root(1)
+        quantise_feat(0)
+        scale_and_shift(1)
+        batch_norm(0, 1)
+        relu_and_regroup(0, 1)
+        transpose_feat(2)
+        quantise_h(0)
+        for g in range(PASSES):
+            batch_norm(1, g)
+
+        def multiply(c):
+            for i in range(SUB):
                 points = slice(i * P, (i + 1) * P)
                 product = product_psum.tile([P, COUT], F32, tag="bank", name="product")
                 for w, (codes, scales) in enumerate((feat_operands[c], h_operands[c])):
@@ -425,21 +421,21 @@ def tile_geoconv_pb_t_kernel(tc, feat, ag, W_feat, b_feat, g1, be1, W_ag, b_ag, 
                 nc.vector.tensor_tensor(out=result[:], in0=products[c, i][:], in1=bias[:], op=ALU.add)
                 nc.sync.dma_start(out=out_chunks[c][:, i, :], in_=result[:])
 
-        halves = (range(SUB // 2), range(SUB // 2, SUB))
+        first_half = range(SUB // 2)
+        second_half = range(SUB // 2, SUB)
         for c in range(N_CHUNKS):
             if c > 0:
                 quantise_h(c)
-                add_bias_and_store(c - 1, halves[1])
-            for g in range(PASSES):
-                if c + FEAT_TURN_AHEAD < N_CHUNKS:
-                    transpose_feat(c + FEAT_TURN_AHEAD, g)
-                multiply(c, halves[g])
-                if c + 2 < N_CHUNKS:
+                add_bias_and_store(c - 1, second_half)
+            if c + FEAT_TURN_AHEAD < N_CHUNKS:
+                transpose_feat(c + FEAT_TURN_AHEAD)
+            multiply(c)
+            if c + 2 < N_CHUNKS:
+                for g in range(PASSES):
                     batch_norm(c + 2, g)
-                if c + 1 < N_CHUNKS:
+            if c + 1 < N_CHUNKS:
+                quantise_feat(c + 1)
+                for g in range(PASSES):
                     relu_and_regroup(c + 1, g)
-                if g == 0:
-                    add_bias_and_store(c, halves[0])
-                    if c + 1 < N_CHUNKS:
-                        quantise_feat(c + 1)
-        add_bias_and_store(N_CHUNKS - 1, halves[1])
+            add_bias_and_store(c, first_half)
+        add_bias_and_store(N_CHUNKS - 1, second_half)

@@ -29,7 +29,7 @@ BN_STATS_DIM = 6
 PSUM_BANKS = 8
 NATURAL_BUFS = 5
 PE_STAT_TILES = PACK
-VECTOR_SUB_TILE = SUB - 1
+VECTOR_SUB_TILES = 1
 VECTOR_SUB_TILE_CHUNKS = 4
 AG_TURN_BANKS = PSUM_BANKS - PE_STAT_TILES - 1
 FEAT_TURN_BANKS = SUB
@@ -70,10 +70,10 @@ def tile_geoconv_pb_t_kernel(tc, feat, ag, W_feat, b_feat, g1, be1, W_ag, b_ag, 
         ident_f32 = keep.tile([P, P], F32)
         make_identity(nc, ident_f32[:])
 
-        minus_half = keep.tile([P, PACK], F32)
-        nc.vector.memset(minus_half[:], -0.5)
-        table_warmer = keep.tile([P, PACK], F32)
-        nc.scalar.activation(out=table_warmer[:], in_=minus_half[:], func=ACT.Relu)
+        eps = keep.tile([P, 1], F32)
+        nc.vector.memset(eps[:], BN_EPS)
+        table_warmer = keep.tile([P, 1], F32)
+        nc.scalar.activation(out=table_warmer[:], in_=eps[:], func=ACT.Sqrt)
 
         ones = keep.tile([P, COUT], BF16)
         nc.vector.memset(ones[:], 1.0)
@@ -120,7 +120,7 @@ def tile_geoconv_pb_t_kernel(tc, feat, ag, W_feat, b_feat, g1, be1, W_ag, b_ag, 
         mean_squared = keep.tile([P, PACK], F32)
         var_1 = keep.tile([P, PACK], F32)
         mean = [mean_var[0][:, :, 0], moments[:, 1, :]]
-        var_eps = [keep.tile([P, PACK], F32, name="var_eps%d" % g) for g in range(PASSES)]
+        std = [keep.tile([P, PACK], F32, name="std%d" % g) for g in range(PASSES)]
         inv_std = [keep.tile([P, PACK], F32, name="inv_std%d" % g) for g in range(PASSES)]
         bn_scale = [keep.tile([P, PACK], F32, name="bn_scale%d" % g) for g in range(PASSES)]
         scaled_mean = [keep.tile([P, PACK], F32, name="scaled_mean%d" % g) for g in range(PASSES)]
@@ -189,10 +189,11 @@ def tile_geoconv_pb_t_kernel(tc, feat, ag, W_feat, b_feat, g1, be1, W_ag, b_ag, 
             )
             feat_operands[c] = (feat_codes, feat_scales)
 
-        def one_over_root(g):
-            nc.gpsimd.tensor_tensor(out=inv_std[g][:], in0=var_eps[g][:], in1=minus_half[:], op=ALU.pow)
+        def root(g, var):
+            nc.scalar.activation(out=std[g][:], in_=var, func=ACT.Sqrt, bias=eps[:], scale=1.0)
 
         def scale_and_shift(g):
+            nc.vector.reciprocal(out=inv_std[g][:], in_=std[g][:])
             nc.vector.tensor_mul(out=bn_scale[g][:], in0=gain_shift[:, 0, g, :], in1=inv_std[g][:])
             nc.vector.tensor_mul(out=scaled_mean[g][:], in0=mean[g], in1=bn_scale[g][:])
             nc.vector.tensor_sub(out=bn_shift[g][:], in0=gain_shift[:, 1, g, :], in1=scaled_mean[g][:])
@@ -238,7 +239,7 @@ def tile_geoconv_pb_t_kernel(tc, feat, ag, W_feat, b_feat, g1, be1, W_ag, b_ag, 
                 (c, i)
                 for c in range(N_CHUNKS)
                 for i in range(SUB)
-                if c >= VECTOR_SUB_TILE_CHUNKS or i != VECTOR_SUB_TILE
+                if c >= VECTOR_SUB_TILE_CHUNKS or i < SUB - VECTOR_SUB_TILES
             ]
             pe_blocks = len(pe_order)
             turned = part1.enter_context(tc.psum_pool(name="turned", bufs=AG_TURN_BANKS))
@@ -254,8 +255,8 @@ def tile_geoconv_pb_t_kernel(tc, feat, ag, W_feat, b_feat, g1, be1, W_ag, b_ag, 
 
             def group_weight(w, g):
                 nc.gpsimd.tensor_scalar(
-                    out=by_runs_dst(w_grouped[:, w, g, :, :]),
-                    in0=by_runs_src(w_rows[w][:, g * PACK : (g + 1) * PACK, :]),
+                    out=w_grouped[:, w, g, :, :],
+                    in0=w_rows[w][:, g * PACK : (g + 1) * PACK, :].rearrange("p t n -> p n t"),
                     scalar1=1.0,
                     scalar2=0.0,
                     op0=ALU.mult,
@@ -277,20 +278,23 @@ def tile_geoconv_pb_t_kernel(tc, feat, ag, W_feat, b_feat, g1, be1, W_ag, b_ag, 
             for c in range(N_CHUNKS):
                 ag_nat = loaded[c]
                 for q in range(PACK):
+                    bank = turned.tile([P, 2, SUB, P], BF16, tag="bank")
                     for j in (2 * q, 2 * q + 1):
                         g, t = divmod(j, PACK)
-                        bank = turned.tile([P, SUB, P], BF16, tag="bank")
                         for i in range(SUB):
                             every_4th = ag_nat[:, i, g * K_PASS + t : (g + 1) * K_PASS : PACK]
-                            nc.tensor.transpose(bank[:, i, :], every_4th, ident_bf16[:])
-                        nc.scalar.copy(
-                            out=ag_t[c][:, j, :].bitcast(F32), in_=bank[:].rearrange("p i q -> p (i q)").bitcast(F32)
-                        )
+                            nc.tensor.transpose(bank[:, j % 2, i, :], every_4th, ident_bf16[:])
+                    nc.scalar.copy(
+                        out=ag_t[c][:, 2 * q : 2 * q + 2, :].rearrange("p j n -> p (j n)").bitcast(F32),
+                        in_=bank[:].rearrange("p j i q -> p (j i q)").bitcast(F32),
+                    )
+                    for j in (2 * q, 2 * q + 1):
+                        g, t = divmod(j, PACK)
                         if g == 0:
                             nc.vector.bn_stats(out=stats[0][:, t, c, :], in_=ag_t[c][:, j, :])
                         elif c < VECTOR_SUB_TILE_CHUNKS:
-                            sub_tile = slice(VECTOR_SUB_TILE * P, (VECTOR_SUB_TILE + 1) * P)
-                            nc.vector.bn_stats(out=stats[1][:, t, c, :], in_=ag_t[c][:, j, sub_tile])
+                            last = slice((SUB - VECTOR_SUB_TILES) * P, CHUNK)
+                            nc.vector.bn_stats(out=stats[1][:, t, c, :], in_=ag_t[c][:, j, last])
                     for i in range(SUB):
                         if (c, i) not in pe_order:
                             continue
@@ -306,8 +310,8 @@ def tile_geoconv_pb_t_kernel(tc, feat, ag, W_feat, b_feat, g1, be1, W_ag, b_ag, 
                             start=True,
                             stop=True,
                         )
-                if c == VECTOR_SUB_TILE_CHUNKS:
-                    share = VECTOR_SUB_TILE_CHUNKS * P / POINTS
+                if c == min(VECTOR_SUB_TILE_CHUNKS, N_CHUNKS - 1):
+                    share = VECTOR_SUB_TILE_CHUNKS * VECTOR_SUB_TILES * P / POINTS
                     for t in range(PACK):
                         nc.vector.bn_aggr(
                             out=mean_var[1][:, t, :], in_=stats[1][:, t, :, :].rearrange("p c s -> p (c s)")
@@ -333,8 +337,6 @@ def tile_geoconv_pb_t_kernel(tc, feat, ag, W_feat, b_feat, g1, be1, W_ag, b_ag, 
 
             for t in range(PACK):
                 nc.vector.bn_aggr(out=mean_var[0][:, t, :], in_=stats[0][:, t, :, :].rearrange("p c s -> p (c s)"))
-            nc.vector.tensor_scalar_add(out=var_eps[0][:], in0=mean_var[0][:, :, 1], scalar1=BN_EPS)
-            one_over_root(0)
             for q in range(PE_STAT_TILES):
                 nc.vector.scalar_tensor_tensor(
                     out=diagonal[:, q, :],
@@ -354,9 +356,9 @@ def tile_geoconv_pb_t_kernel(tc, feat, ag, W_feat, b_feat, g1, be1, W_ag, b_ag, 
         turned = ctx.enter_context(tc.psum_pool(name="feat_turned", bufs=FEAT_TURN_BANKS, reuse_waits="tile"))
         product_psum = ctx.enter_context(tc.psum_pool(name="product_psum", bufs=PRODUCT_BANKS, reuse_waits="tile"))
 
+        root(0, mean_var[0][:, :, 1])
         transpose_feat(0)
         keep_clock_up(product_psum, 2)
-        transpose_feat(1)
         scale_and_shift(0)
         batch_norm(0, 0)
         relu_and_regroup(0, 0)
@@ -385,10 +387,9 @@ def tile_geoconv_pb_t_kernel(tc, feat, ag, W_feat, b_feat, g1, be1, W_ag, b_ag, 
         nc.vector.tensor_add(out=moments[:], in0=moments[:], in1=vector_moments[:])
         nc.vector.tensor_mul(out=mean_squared[:], in0=mean[1], in1=mean[1])
         nc.vector.tensor_sub(out=var_1[:], in0=moments[:, 0, :], in1=mean_squared[:])
-        nc.vector.tensor_scalar(
-            out=var_eps[1][:], in0=var_1[:], scalar1=0.0, scalar2=BN_EPS, op0=ALU.max, op1=ALU.add
-        )
-        one_over_root(1)
+        nc.vector.tensor_scalar_max(out=var_1[:], in0=var_1[:], scalar1=0.0)
+        root(1, var_1[:])
+        transpose_feat(1)
         quantise_feat(0)
         scale_and_shift(1)
         batch_norm(0, 1)

@@ -35,7 +35,7 @@ AG_TURN_BANKS = PSUM_BANKS - PE_STAT_TILES - 1
 FEAT_TURN_BANKS = SUB
 PRODUCT_BANKS = PSUM_BANKS - FEAT_TURN_BANKS
 WEIGHT_CHUNKS = (5, 6)
-SUM_COLUMNS = 16
+SUM_COLUMNS = 48
 WARM_UP_MATMULS = 6
 FEAT_TURN_AHEAD = 3
 VECTOR_REGROUPS_EVERY = 4
@@ -277,39 +277,40 @@ def tile_geoconv_pb_t_kernel(tc, feat, ag, W_feat, b_feat, g1, be1, W_ag, b_ag, 
             keep_clock_up(turned, WARM_UP_MATMULS)
             for c in range(N_CHUNKS):
                 ag_nat = loaded[c]
-                for q in range(PACK):
-                    bank = turned.tile([P, 2, SUB, P], BF16, tag="bank")
-                    for j in (2 * q, 2 * q + 1):
-                        g, t = divmod(j, PACK)
+                for g in range(PASSES):
+                    for t in range(0, PACK, 2):
+                        bank = turned.tile([P, 2, SUB, P], BF16, tag="bank")
+                        for k in range(2):
+                            for i in range(SUB):
+                                every_4th = ag_nat[:, i, g * K_PASS + t + k : (g + 1) * K_PASS : PACK]
+                                nc.tensor.transpose(bank[:, k, i, :], every_4th, ident_bf16[:])
+                        j = g * PACK + t
+                        nc.scalar.copy(
+                            out=ag_t[c][:, j : j + 2, :].rearrange("p j n -> p (j n)").bitcast(F32),
+                            in_=bank[:].rearrange("p j i q -> p (j i q)").bitcast(F32),
+                        )
+                        for k in range(2):
+                            if g == 0:
+                                nc.vector.bn_stats(out=stats[0][:, t + k, c, :], in_=ag_t[c][:, j + k, :])
+                            elif c < VECTOR_SUB_TILE_CHUNKS:
+                                last = slice((SUB - VECTOR_SUB_TILES) * P, CHUNK)
+                                nc.vector.bn_stats(out=stats[1][:, t + k, c, :], in_=ag_t[c][:, j + k, last])
+                    for q in (2 * g, 2 * g + 1):
                         for i in range(SUB):
-                            every_4th = ag_nat[:, i, g * K_PASS + t : (g + 1) * K_PASS : PACK]
-                            nc.tensor.transpose(bank[:, j % 2, i, :], every_4th, ident_bf16[:])
-                    nc.scalar.copy(
-                        out=ag_t[c][:, 2 * q : 2 * q + 2, :].rearrange("p j n -> p (j n)").bitcast(F32),
-                        in_=bank[:].rearrange("p j i q -> p (j i q)").bitcast(F32),
-                    )
-                    for j in (2 * q, 2 * q + 1):
-                        g, t = divmod(j, PACK)
-                        if g == 0:
-                            nc.vector.bn_stats(out=stats[0][:, t, c, :], in_=ag_t[c][:, j, :])
-                        elif c < VECTOR_SUB_TILE_CHUNKS:
-                            last = slice((SUB - VECTOR_SUB_TILES) * P, CHUNK)
-                            nc.vector.bn_stats(out=stats[1][:, t, c, :], in_=ag_t[c][:, j, last])
-                    for i in range(SUB):
-                        if (c, i) not in pe_order:
-                            continue
-                        block = ag_nat[:, i, K_PASS + q * P : K_PASS + (q + 1) * P]
-                        b = pe_order.index((c, i))
-                        nc.tensor.matmul(
-                            out=squares[q][:], lhsT=block, rhs=block, start=(b == 0), stop=(b == pe_blocks - 1)
-                        )
-                        nc.tensor.matmul(
-                            out=values[:, q, 2 * b : 2 * b + SUM_COLUMNS],
-                            lhsT=block,
-                            rhs=ones[:, 0:SUM_COLUMNS],
-                            start=True,
-                            stop=True,
-                        )
+                            if (c, i) not in pe_order:
+                                continue
+                            block = ag_nat[:, i, K_PASS + q * P : K_PASS + (q + 1) * P]
+                            b = pe_order.index((c, i))
+                            nc.tensor.matmul(
+                                out=squares[q][:], lhsT=block, rhs=block, start=(b == 0), stop=(b == pe_blocks - 1)
+                            )
+                            nc.tensor.matmul(
+                                out=values[:, q, 2 * b : 2 * b + SUM_COLUMNS],
+                                lhsT=block,
+                                rhs=ones[:, 0:SUM_COLUMNS],
+                                start=True,
+                                stop=True,
+                            )
                 if c == min(VECTOR_SUB_TILE_CHUNKS, N_CHUNKS - 1):
                     share = VECTOR_SUB_TILE_CHUNKS * VECTOR_SUB_TILES * P / POINTS
                     for t in range(PACK):

@@ -29,16 +29,13 @@ BN_STATS_DIM = 6
 PSUM_BANKS = 8
 NATURAL_BUFS = 5
 PE_STAT_TILES = PACK
-VECTOR_SUB_TILES = 1
-VECTOR_SUB_TILE_CHUNKS = 4
 AG_TURN_BANKS = PSUM_BANKS - PE_STAT_TILES - 1
 FEAT_TURN_BANKS = SUB
 PRODUCT_BANKS = PSUM_BANKS - FEAT_TURN_BANKS
-WEIGHT_CHUNKS = (5, 6)
-SUM_COLUMNS = 48
+WEIGHT_CHUNKS = (4, 5)
+SUM_COLUMNS = 32
 WARM_UP_MATMULS = 6
 FEAT_TURN_AHEAD = 3
-VECTOR_REGROUPS_EVERY = 4
 RUN = 4
 
 FLOPS = 2 * POINTS * (CHANNELS + CHANNELS) * COUT
@@ -102,24 +99,23 @@ def tile_geoconv_pb_t_kernel(tc, feat, ag, W_feat, b_feat, g1, be1, W_ag, b_ag, 
         )
         bias = keep.tile([P, COUT], F32)
 
-        ag_t = [keep.tile([P, PASSES * PACK, CHUNK], BF16, name="ag_t%d" % c) for c in range(N_CHUNKS)]
+        ag_words = [keep.tile([P, 2 * PASSES, CHUNK], F32, name="ag_words%d" % c) for c in range(N_CHUNKS)]
+
+        def ag_values(c, g, t):
+            return ag_words[c][:, 2 * g + t // 2, :].bitcast(BF16)[:, t % 2 :: 2]
 
         w_codes = keep.tile([P, 2, PASSES, COUT], U32, align_bytes=64)
         w_scales = keep.tile([P, 2, PASSES, COUT], U8, align_bytes=64)
-        stats = [
-            keep.tile([P, PACK, N_CHUNKS, BN_STATS_DIM], F32, name="stats0"),
-            keep.tile([P, PACK, VECTOR_SUB_TILE_CHUNKS, BN_STATS_DIM], F32, name="stats1"),
-        ]
-        mean_var = [keep.tile([P, PACK, 2], F32, name="mean_var%d" % g) for g in range(PASSES)]
+        stats = keep.tile([P, PACK, N_CHUNKS, BN_STATS_DIM], F32)
+        mean_var = keep.tile([P, PACK, 2], F32)
         diagonal = keep.tile([P, PE_STAT_TILES, P], F32)
         sums = keep.tile([P, 2, PE_STAT_TILES], F32)
         sum_of_values = keep.tile([P, PE_STAT_TILES], F32)
         masked = keep.tile([P, 2 * PACK, PACK], F32)
         moments = keep.tile([P, 2, PACK], F32)
-        vector_moments = keep.tile([P, 2, PACK], F32)
         mean_squared = keep.tile([P, PACK], F32)
         var_1 = keep.tile([P, PACK], F32)
-        mean = [mean_var[0][:, :, 0], moments[:, 1, :]]
+        mean = [mean_var[:, :, 0], moments[:, 1, :]]
         std = [keep.tile([P, PACK], F32, name="std%d" % g) for g in range(PASSES)]
         inv_std = [keep.tile([P, PACK], F32, name="inv_std%d" % g) for g in range(PASSES)]
         bn_scale = [keep.tile([P, PACK], F32, name="bn_scale%d" % g) for g in range(PASSES)]
@@ -133,10 +129,15 @@ def tile_geoconv_pb_t_kernel(tc, feat, ag, W_feat, b_feat, g1, be1, W_ag, b_ag, 
         def load_next_chunk():
             if len(loaded) < len(sources):
                 chunk = natural.tile([P, SUB, CHANNELS], BF16, tag="natural", name="chunk")
-                pieces = PASSES if not loaded else 1
-                for piece in range(pieces):
-                    channels = slice(piece * CHANNELS // pieces, (piece + 1) * CHANNELS // pieces)
-                    nc.sync.dma_start(out=chunk[:, :, channels], in_=sources[len(loaded)][:, :, channels])
+                if not loaded:
+                    for g in range(PASSES):
+                        channels = slice(g * K_PASS, (g + 1) * K_PASS)
+                        for i0 in range(0, SUB, 2):
+                            nc.sync.dma_start(
+                                out=chunk[:, i0 : i0 + 2, channels], in_=sources[0][:, i0 : i0 + 2, channels]
+                            )
+                else:
+                    nc.sync.dma_start(out=chunk[:], in_=sources[len(loaded)])
                 loaded.append(chunk)
 
         def load_weight(weight):
@@ -203,7 +204,7 @@ def tile_geoconv_pb_t_kernel(tc, feat, ag, W_feat, b_feat, g1, be1, W_ag, b_ag, 
             for t in range(PACK):
                 nc.vector.tensor_scalar(
                     out=h_normed[c, g][:, t, :],
-                    in0=ag_t[c][:, g * PACK + t, :],
+                    in0=ag_values(c, g, t),
                     scalar1=bn_scale[g][:, t : t + 1],
                     scalar2=bn_shift[g][:, t : t + 1],
                     op0=ALU.mult,
@@ -215,7 +216,7 @@ def tile_geoconv_pb_t_kernel(tc, feat, ag, W_feat, b_feat, g1, be1, W_ag, b_ag, 
                 h_grouped[c] = h_pool.tile([P, PASSES, CHUNK, PACK], BF16, align_bytes=64, name="h_grouped")
             grouped = by_runs_dst(h_grouped[c][:, g, :, :])
             rows = by_runs_src(h_normed[c, g][:])
-            if g == PASSES - 1 and c % VECTOR_REGROUPS_EVERY == 0:
+            if g == PASSES - 1 and c == 0:
                 nc.vector.tensor_scalar_max(out=grouped, in0=rows, scalar1=0.0)
             else:
                 nc.scalar.activation(out=grouped, in_=rows, func=ACT.Relu)
@@ -235,15 +236,9 @@ def tile_geoconv_pb_t_kernel(tc, feat, ag, W_feat, b_feat, g1, be1, W_ag, b_ag, 
             w_stage = part1.enter_context(tc.tile_pool(name="w_stage", bufs=1))
             sums_psum = part1.enter_context(tc.psum_pool(name="sums_psum", bufs=1))
             squares = [sums_psum.tile([P, P], F32, name="squares%d" % s) for s in range(PE_STAT_TILES)]
-            pe_order = [
-                (c, i)
-                for c in range(N_CHUNKS)
-                for i in range(SUB)
-                if c >= VECTOR_SUB_TILE_CHUNKS or i < SUB - VECTOR_SUB_TILES
-            ]
-            pe_blocks = len(pe_order)
+            blocks = N_CHUNKS * SUB
             turned = part1.enter_context(tc.psum_pool(name="turned", bufs=AG_TURN_BANKS))
-            values = sums_psum.tile([P, PE_STAT_TILES, 2 * pe_blocks + SUM_COLUMNS], F32)
+            values = sums_psum.tile([P, PE_STAT_TILES, 2 * blocks + SUM_COLUMNS], F32)
 
             for k in range(NATURAL_BUFS - 2):
                 load_next_chunk()
@@ -277,32 +272,23 @@ def tile_geoconv_pb_t_kernel(tc, feat, ag, W_feat, b_feat, g1, be1, W_ag, b_ag, 
             keep_clock_up(turned, WARM_UP_MATMULS)
             for c in range(N_CHUNKS):
                 ag_nat = loaded[c]
+                nat_words = ag_nat[:].bitcast(F32)
                 for g in range(PASSES):
-                    for t in range(0, PACK, 2):
-                        bank = turned.tile([P, 2, SUB, P], BF16, tag="bank")
-                        for k in range(2):
-                            for i in range(SUB):
-                                every_4th = ag_nat[:, i, g * K_PASS + t + k : (g + 1) * K_PASS : PACK]
-                                nc.tensor.transpose(bank[:, k, i, :], every_4th, ident_bf16[:])
-                        j = g * PACK + t
-                        nc.scalar.copy(
-                            out=ag_t[c][:, j : j + 2, :].rearrange("p j n -> p (j n)").bitcast(F32),
-                            in_=bank[:].rearrange("p j i q -> p (j i q)").bitcast(F32),
-                        )
-                        for k in range(2):
-                            if g == 0:
-                                nc.vector.bn_stats(out=stats[0][:, t + k, c, :], in_=ag_t[c][:, j + k, :])
-                            elif c < VECTOR_SUB_TILE_CHUNKS:
-                                last = slice((SUB - VECTOR_SUB_TILES) * P, CHUNK)
-                                nc.vector.bn_stats(out=stats[1][:, t + k, c, :], in_=ag_t[c][:, j + k, last])
+                    for u in range(2):
+                        bank = turned.tile([P, SUB, P], F32, tag="bank")
+                        for i in range(SUB):
+                            every_2nd = nat_words[:, i, 2 * g * P + u : 2 * (g + 1) * P : 2]
+                            nc.tensor.transpose(bank[:, i, :], every_2nd, ident_f32[:])
+                        nc.scalar.copy(out=ag_words[c][:, 2 * g + u, :], in_=bank[:].rearrange("p i q -> p (i q)"))
+                        if g == 0:
+                            for t in (2 * u, 2 * u + 1):
+                                nc.vector.bn_stats(out=stats[:, t, c, :], in_=ag_values(c, g, t))
                     for q in (2 * g, 2 * g + 1):
                         for i in range(SUB):
-                            if (c, i) not in pe_order:
-                                continue
                             block = ag_nat[:, i, K_PASS + q * P : K_PASS + (q + 1) * P]
-                            b = pe_order.index((c, i))
+                            b = c * SUB + i
                             nc.tensor.matmul(
-                                out=squares[q][:], lhsT=block, rhs=block, start=(b == 0), stop=(b == pe_blocks - 1)
+                                out=squares[q][:], lhsT=block, rhs=block, start=(b == 0), stop=(b == blocks - 1)
                             )
                             nc.tensor.matmul(
                                 out=values[:, q, 2 * b : 2 * b + SUM_COLUMNS],
@@ -311,16 +297,6 @@ def tile_geoconv_pb_t_kernel(tc, feat, ag, W_feat, b_feat, g1, be1, W_ag, b_ag, 
                                 start=True,
                                 stop=True,
                             )
-                if c == min(VECTOR_SUB_TILE_CHUNKS, N_CHUNKS - 1):
-                    share = VECTOR_SUB_TILE_CHUNKS * VECTOR_SUB_TILES * P / POINTS
-                    for t in range(PACK):
-                        nc.vector.bn_aggr(
-                            out=mean_var[1][:, t, :], in_=stats[1][:, t, :, :].rearrange("p c s -> p (c s)")
-                        )
-                    nc.vector.tensor_mul(out=mean_squared[:], in0=mean_var[1][:, :, 0], in1=mean_var[1][:, :, 0])
-                    nc.vector.tensor_add(out=var_1[:], in0=mean_squared[:], in1=mean_var[1][:, :, 1])
-                    nc.vector.tensor_scalar_mul(out=vector_moments[:, 0, :], in0=var_1[:], scalar1=share)
-                    nc.vector.tensor_scalar_mul(out=vector_moments[:, 1, :], in0=mean_var[1][:, :, 0], scalar1=share)
                 if c in WEIGHT_CHUNKS:
                     quantise_weight(WEIGHT_CHUNKS.index(c))
                 load_next_chunk()
@@ -337,7 +313,7 @@ def tile_geoconv_pb_t_kernel(tc, feat, ag, W_feat, b_feat, g1, be1, W_ag, b_ag, 
             nc.scalar.copy(out=bias[:], in_=bias_sum[:])
 
             for t in range(PACK):
-                nc.vector.bn_aggr(out=mean_var[0][:, t, :], in_=stats[0][:, t, :, :].rearrange("p c s -> p (c s)"))
+                nc.vector.bn_aggr(out=mean_var[:, t, :], in_=stats[:, t, :, :].rearrange("p c s -> p (c s)"))
             for q in range(PE_STAT_TILES):
                 nc.vector.scalar_tensor_tensor(
                     out=diagonal[:, q, :],
@@ -349,7 +325,7 @@ def tile_geoconv_pb_t_kernel(tc, feat, ag, W_feat, b_feat, g1, be1, W_ag, b_ag, 
                     accum_out=sums[:, 0, q : q + 1],
                 )
             nc.vector.tensor_reduce(
-                out=sum_of_values[:], in_=values[:, :, 0 : 2 * pe_blocks : 2], axis=AXIS.X, op=ALU.add
+                out=sum_of_values[:], in_=values[:, :, 0 : 2 * blocks : 2], axis=AXIS.X, op=ALU.add
             )
             nc.vector.tensor_scalar_mul(out=sums[:, 1, :], in0=sum_of_values[:], scalar1=1.0 / POINTS)
 
@@ -357,7 +333,7 @@ def tile_geoconv_pb_t_kernel(tc, feat, ag, W_feat, b_feat, g1, be1, W_ag, b_ag, 
         turned = ctx.enter_context(tc.psum_pool(name="feat_turned", bufs=FEAT_TURN_BANKS, reuse_waits="tile"))
         product_psum = ctx.enter_context(tc.psum_pool(name="product_psum", bufs=PRODUCT_BANKS, reuse_waits="tile"))
 
-        root(0, mean_var[0][:, :, 1])
+        root(0, mean_var[:, :, 1])
         transpose_feat(0)
         keep_clock_up(product_psum, 2)
         scale_and_shift(0)
@@ -385,7 +361,6 @@ def tile_geoconv_pb_t_kernel(tc, feat, ag, W_feat, b_feat, g1, be1, W_ag, b_ag, 
             axis=AXIS.X,
             op=ALU.add,
         )
-        nc.vector.tensor_add(out=moments[:], in0=moments[:], in1=vector_moments[:])
         nc.vector.tensor_mul(out=mean_squared[:], in0=mean[1], in1=mean[1])
         nc.vector.tensor_sub(out=var_1[:], in0=moments[:, 0, :], in1=mean_squared[:])
         nc.vector.tensor_scalar_max(out=var_1[:], in0=var_1[:], scalar1=0.0)

@@ -29,11 +29,13 @@ BN_STATS_DIM = 6
 PSUM_BANKS = 8
 NATURAL_BUFS = 5
 PE_STAT_TILES = PACK
-AG_TURN_BANKS = PSUM_BANKS - PE_STAT_TILES - 1
+AG_TURN_BANKS = PSUM_BANKS - PE_STAT_TILES
 FEAT_TURN_BANKS = SUB
 PRODUCT_BANKS = PSUM_BANKS - FEAT_TURN_BANKS
+VECTOR_REGROUPS = (0, 2)
+SMALL_VECTORS_CHUNK = 2
 WEIGHT_CHUNKS = (4, 5)
-SUM_COLUMNS = 32
+SQUARE_COLUMNS = 144
 WARM_UP_MATMULS = 6
 FEAT_TURN_AHEAD = 3
 RUN = 4
@@ -99,23 +101,28 @@ def tile_geoconv_pb_t_kernel(tc, feat, ag, W_feat, b_feat, g1, be1, W_ag, b_ag, 
         )
         bias = keep.tile([P, COUT], F32)
 
-        ag_words = [keep.tile([P, 2 * PASSES, CHUNK], F32, name="ag_words%d" % c) for c in range(N_CHUNKS)]
+        ag_words = [keep.tile([P, 2, CHUNK], F32, name="ag_words%d" % c) for c in range(N_CHUNKS)]
+        ag_rows = [keep.tile([P, PACK, CHUNK], BF16, name="ag_rows%d" % c) for c in range(N_CHUNKS)]
 
         def ag_values(c, g, t):
-            return ag_words[c][:, 2 * g + t // 2, :].bitcast(BF16)[:, t % 2 :: 2]
+            if g == 0:
+                return ag_words[c][:, t // 2, :].bitcast(BF16)[:, t % 2 :: 2]
+            return ag_rows[c][:, t, :]
 
         w_codes = keep.tile([P, 2, PASSES, COUT], U32, align_bytes=64)
         w_scales = keep.tile([P, 2, PASSES, COUT], U8, align_bytes=64)
         stats = keep.tile([P, PACK, N_CHUNKS, BN_STATS_DIM], F32)
         mean_var = keep.tile([P, PACK, 2], F32)
         diagonal = keep.tile([P, PE_STAT_TILES, P], F32)
-        sums = keep.tile([P, 2, PE_STAT_TILES], F32)
-        sum_of_values = keep.tile([P, PE_STAT_TILES], F32)
-        masked = keep.tile([P, 2 * PACK, PACK], F32)
-        moments = keep.tile([P, 2, PACK], F32)
+        squares_mean = keep.tile([P, PE_STAT_TILES], F32)
+        row_sums = keep.tile([P, PACK, N_CHUNKS], F32)
+        row_sum = keep.tile([P, PACK], F32)
+        masked = keep.tile([P, PACK, PACK], F32)
+        mean_of_squares = keep.tile([P, PACK], F32)
+        mean_1 = keep.tile([P, PACK], F32)
         mean_squared = keep.tile([P, PACK], F32)
         var_1 = keep.tile([P, PACK], F32)
-        mean = [mean_var[:, :, 0], moments[:, 1, :]]
+        mean = [mean_var[:, :, 0], mean_1[:]]
         std = [keep.tile([P, PACK], F32, name="std%d" % g) for g in range(PASSES)]
         inv_std = [keep.tile([P, PACK], F32, name="inv_std%d" % g) for g in range(PASSES)]
         bn_scale = [keep.tile([P, PACK], F32, name="bn_scale%d" % g) for g in range(PASSES)]
@@ -216,7 +223,7 @@ def tile_geoconv_pb_t_kernel(tc, feat, ag, W_feat, b_feat, g1, be1, W_ag, b_ag, 
                 h_grouped[c] = h_pool.tile([P, PASSES, CHUNK, PACK], BF16, align_bytes=64, name="h_grouped")
             grouped = by_runs_dst(h_grouped[c][:, g, :, :])
             rows = by_runs_src(h_normed[c, g][:])
-            if g == PASSES - 1 and c == 0:
+            if g == PASSES - 1 and c in VECTOR_REGROUPS:
                 nc.vector.tensor_scalar_max(out=grouped, in0=rows, scalar1=0.0)
             else:
                 nc.scalar.activation(out=grouped, in_=rows, func=ACT.Relu)
@@ -234,11 +241,12 @@ def tile_geoconv_pb_t_kernel(tc, feat, ag, W_feat, b_feat, g1, be1, W_ag, b_ag, 
 
         with ExitStack() as part1:
             w_stage = part1.enter_context(tc.tile_pool(name="w_stage", bufs=1))
-            sums_psum = part1.enter_context(tc.psum_pool(name="sums_psum", bufs=1))
-            squares = [sums_psum.tile([P, P], F32, name="squares%d" % s) for s in range(PE_STAT_TILES)]
-            blocks = N_CHUNKS * SUB
             turned = part1.enter_context(tc.psum_pool(name="turned", bufs=AG_TURN_BANKS))
-            values = sums_psum.tile([P, PE_STAT_TILES, 2 * blocks + SUM_COLUMNS], F32)
+            sums_psum = part1.enter_context(tc.psum_pool(name="sums_psum", bufs=1))
+            squares = [
+                sums_psum.tile([P, SQUARE_COLUMNS], F32, name="squares%d" % q) for q in range(PE_STAT_TILES)
+            ]
+            blocks = N_CHUNKS * SUB
 
             for k in range(NATURAL_BUFS - 2):
                 load_next_chunk()
@@ -279,55 +287,61 @@ def tile_geoconv_pb_t_kernel(tc, feat, ag, W_feat, b_feat, g1, be1, W_ag, b_ag, 
                         for i in range(SUB):
                             every_2nd = nat_words[:, i, 2 * g * P + u : 2 * (g + 1) * P : 2]
                             nc.tensor.transpose(bank[:, i, :], every_2nd, ident_f32[:])
-                        nc.scalar.copy(out=ag_words[c][:, 2 * g + u, :], in_=bank[:].rearrange("p i q -> p (i q)"))
+                        turned_words = bank[:].rearrange("p i q -> p (i q)")
                         if g == 0:
-                            for t in (2 * u, 2 * u + 1):
-                                nc.vector.bn_stats(out=stats[:, t, c, :], in_=ag_values(c, g, t))
+                            nc.scalar.copy(out=ag_words[c][:, u, :], in_=turned_words)
+                            if u == 1:
+                                for t in range(PACK):
+                                    nc.vector.bn_stats(out=stats[:, t, c, :], in_=ag_values(c, g, t))
+                        else:
+                            for e in range(2):
+                                t = 2 * u + e
+                                nc.scalar.activation(
+                                    out=ag_rows[c][:, t, :],
+                                    in_=turned_words.bitcast(BF16)[:, e::2],
+                                    func=ACT.Copy,
+                                    accum_out=row_sums[:, t, c : c + 1],
+                                )
                     for q in (2 * g, 2 * g + 1):
                         for i in range(SUB):
-                            block = ag_nat[:, i, K_PASS + q * P : K_PASS + (q + 1) * P]
+                            end = K_PASS + (q + 1) * P
+                            block = ag_nat[:, i, end - P : end]
                             b = c * SUB + i
                             nc.tensor.matmul(
-                                out=squares[q][:], lhsT=block, rhs=block, start=(b == 0), stop=(b == blocks - 1)
-                            )
-                            nc.tensor.matmul(
-                                out=values[:, q, 2 * b : 2 * b + SUM_COLUMNS],
+                                out=squares[q][:],
                                 lhsT=block,
-                                rhs=ones[:, 0:SUM_COLUMNS],
-                                start=True,
-                                stop=True,
+                                rhs=ag_nat[:, i, end - SQUARE_COLUMNS : end],
+                                start=(b == 0),
+                                stop=(b == blocks - 1),
                             )
+                if c == SMALL_VECTORS_CHUNK:
+                    vector_cols = turned.tile([P, PACK, P], BF16, tag="bank")
+                    for t in range(PACK):
+                        nc.tensor.transpose(vector_cols[:, t, :], vector_rows[:, t::PACK], ident_bf16[:])
+                    nc.scalar.copy(
+                        out=gain_shift[:].rearrange("p v g t -> p (v g) t"),
+                        in_=vector_cols[:, :, 0 : 2 * PASSES].rearrange("p t r -> p r t"),
+                    )
+                    bias_sum = turned.tile([P, COUT], F32, tag="bank")
+                    nc.tensor.matmul(out=bias_sum[:], lhsT=ones[:, 0:P], rhs=bias_rows[:], start=True, stop=True)
+                    nc.scalar.copy(out=bias[:], in_=bias_sum[:])
                 if c in WEIGHT_CHUNKS:
                     quantise_weight(WEIGHT_CHUNKS.index(c))
                 load_next_chunk()
-
-            vector_cols = turned.tile([P, PACK, P], BF16, tag="bank")
-            for t in range(PACK):
-                nc.tensor.transpose(vector_cols[:, t, :], vector_rows[:, t::PACK], ident_bf16[:])
-            nc.scalar.copy(
-                out=gain_shift[:].rearrange("p v g t -> p (v g) t"),
-                in_=vector_cols[:, :, 0 : 2 * PASSES].rearrange("p t r -> p r t"),
-            )
-            bias_sum = turned.tile([P, COUT], F32, tag="bank")
-            nc.tensor.matmul(out=bias_sum[:], lhsT=ones[:, 0:P], rhs=bias_rows[:], start=True, stop=True)
-            nc.scalar.copy(out=bias[:], in_=bias_sum[:])
 
             for t in range(PACK):
                 nc.vector.bn_aggr(out=mean_var[:, t, :], in_=stats[:, t, :, :].rearrange("p c s -> p (c s)"))
             for q in range(PE_STAT_TILES):
                 nc.vector.scalar_tensor_tensor(
                     out=diagonal[:, q, :],
-                    in0=squares[q][:],
+                    in0=squares[q][:, SQUARE_COLUMNS - P : SQUARE_COLUMNS],
                     scalar=1.0 / POINTS,
                     in1=ident_f32[:],
                     op0=ALU.mult,
                     op1=ALU.mult,
-                    accum_out=sums[:, 0, q : q + 1],
+                    accum_out=squares_mean[:, q : q + 1],
                 )
-            nc.vector.tensor_reduce(
-                out=sum_of_values[:], in_=values[:, :, 0 : 2 * blocks : 2], axis=AXIS.X, op=ALU.add
-            )
-            nc.vector.tensor_scalar_mul(out=sums[:, 1, :], in0=sum_of_values[:], scalar1=1.0 / POINTS)
+            nc.vector.tensor_reduce(out=row_sum[:], in_=row_sums[:], axis=AXIS.X, op=ALU.add)
 
         result_pool = ctx.enter_context(tc.tile_pool(name="result_pool", bufs=8, reuse_waits="tile"))
         turned = ctx.enter_context(tc.psum_pool(name="feat_turned", bufs=FEAT_TURN_BANKS, reuse_waits="tile"))
@@ -339,30 +353,23 @@ def tile_geoconv_pb_t_kernel(tc, feat, ag, W_feat, b_feat, g1, be1, W_ag, b_ag, 
         scale_and_shift(0)
         batch_norm(0, 0)
         relu_and_regroup(0, 0)
-        moved = product_psum.tile([P, PACK, 2, PACK], F32, tag="bank")
+        moved = product_psum.tile([P, PACK, PACK], F32, tag="bank")
         for t in range(PACK):
             nc.tensor.matmul(
-                out=moved[:, t, :, :].rearrange("p v q -> p (v q)"),
+                out=moved[:, t, :],
                 lhsT=select[:, t, :, :].rearrange("p q c -> p (q c)"),
-                rhs=sums[:].rearrange("p v q -> p (v q)"),
+                rhs=squares_mean[:],
                 start=True,
                 stop=True,
             )
         keep_clock_up(product_psum, 2)
+        nc.vector.tensor_scalar_mul(out=mean_1[:], in0=row_sum[:], scalar1=1.0 / POINTS)
         nc.vector.tensor_tensor(
-            out=masked[:],
-            in0=moved[:].rearrange("p t v q -> p (t v) q"),
-            in1=quarter[:].unsqueeze(1).to_broadcast([P, 2 * PACK, PACK]),
-            op=ALU.mult,
+            out=masked[:], in0=moved[:], in1=quarter[:].unsqueeze(1).to_broadcast([P, PACK, PACK]), op=ALU.mult
         )
-        nc.vector.tensor_reduce(
-            out=moments[:].rearrange("p v t -> p t v"),
-            in_=masked[:].rearrange("p (t v) q -> p t v q", v=2),
-            axis=AXIS.X,
-            op=ALU.add,
-        )
-        nc.vector.tensor_mul(out=mean_squared[:], in0=mean[1], in1=mean[1])
-        nc.vector.tensor_sub(out=var_1[:], in0=moments[:, 0, :], in1=mean_squared[:])
+        nc.vector.tensor_mul(out=mean_squared[:], in0=mean_1[:], in1=mean_1[:])
+        nc.vector.tensor_reduce(out=mean_of_squares[:], in_=masked[:], axis=AXIS.X, op=ALU.add)
+        nc.vector.tensor_sub(out=var_1[:], in0=mean_of_squares[:], in1=mean_squared[:])
         nc.vector.tensor_scalar_max(out=var_1[:], in0=var_1[:], scalar1=0.0)
         root(1, var_1[:])
         transpose_feat(1)

from contextlib import ExitStack

import concourse.mybir as mybir
from concourse.masks import make_identity

BF16 = mybir.dt.bfloat16
F32 = mybir.dt.float32
U32 = mybir.dt.uint32
U8 = mybir.dt.uint8
FP8X4 = mybir.dt.float8_e4m3fn_x4
ALU = mybir.AluOpType
ACT = mybir.ActivationFunctionType
AXIS = mybir.AxisListType

P = 128
PACK = 4
K_PASS = P * PACK

POINTS = 8 * 512
CHANNELS = 1024
COUT = 512
BN_EPS = 1e-5

SUB = 4
CHUNK = P * SUB
N_CHUNKS = POINTS // CHUNK
PASSES = CHANNELS // K_PASS
BN_STATS_DIM = 6
PSUM_BANKS = 8
NATURAL_BUFS = 5
PE_STAT_TILES = PACK
AG_TURN_BANKS = PSUM_BANKS - PE_STAT_TILES
FEAT_TURN_BANKS = SUB
PRODUCT_BANKS = PSUM_BANKS - FEAT_TURN_BANKS
VECTOR_REGROUPS = (0, 2)
SMALL_VECTORS_CHUNK = 2
WEIGHT_CHUNKS = (4, 5)
SQUARE_COLUMNS = 144
WARM_UP_MATMULS = 6
FEAT_TURN_AHEAD = 3
RUN = 4

FLOPS = 2 * POINTS * (CHANNELS + CHANNELS) * COUT


def by_runs_src(rows):
    return rows.rearrange("p t (c i) -> p c t i", i=RUN)


def by_runs_dst(grouped):
    return grouped.rearrange("p (c i) t -> p c t i", i=RUN)


def tile_geoconv_pb_t_kernel(tc, feat, ag, W_feat, b_feat, g1, be1, W_ag, b_ag, out):
    nc = tc.nc
    feat_chunks = feat.flatten_outer_dims().rearrange("(c p i) k -> c p i k", p=P, i=SUB)
    ag_chunks = ag.flatten_outer_dims().rearrange("(c p i) k -> c p i k", p=P, i=SUB)
    out_chunks = out.flatten_outer_dims().rearrange("(c p i) n -> c p i n", p=P, i=SUB)

    with ExitStack() as ctx:
        ctx.enter_context(tc.manual_schedule())
        keep = ctx.enter_context(tc.tile_pool(name="keep", bufs=1))
        feat_pool = ctx.enter_context(tc.tile_pool(name="feat_pool", bufs=3))
        h_pool = ctx.enter_context(tc.tile_pool(name="h_pool", bufs=2))
        natural = ctx.enter_context(tc.tile_pool(name="natural", bufs=NATURAL_BUFS, side="right"))

        ident_bf16 = keep.tile([P, P], BF16)
        make_identity(nc, ident_bf16[:])
        ident_f32 = keep.tile([P, P], F32)
        make_identity(nc, ident_f32[:])

        eps = keep.tile([P, 1], F32)
        nc.vector.memset(eps[:], BN_EPS)
        table_warmer = keep.tile([P, 1], F32)
        nc.scalar.activation(out=table_warmer[:], in_=eps[:], func=ACT.Sqrt)

        ones = keep.tile([P, COUT], BF16)
        nc.vector.memset(ones[:], 1.0)
        vector_rows = keep.tile([P, K_PASS], BF16)
        nc.vector.memset(vector_rows[:], 0.0)
        nc.scalar.dma_start(out=vector_rows[0:PASSES, :], in_=g1.rearrange("(g k) -> g k", g=PASSES))
        nc.scalar.dma_start(out=vector_rows[PASSES : 2 * PASSES, :], in_=be1.rearrange("(g k) -> g k", g=PASSES))
        bias_rows = keep.tile([P, COUT], BF16)
        nc.vector.memset(bias_rows[:], 0.0)
        nc.scalar.dma_start(out=bias_rows[0:1, :], in_=b_feat.rearrange("(o n) -> o n", o=1))
        nc.scalar.dma_start(out=bias_rows[1:2, :], in_=b_ag.rearrange("(o n) -> o n", o=1))
        gain_shift = keep.tile([P, 2, PASSES, PACK], F32)
        select = keep.tile([P, PACK, PACK, P // PACK], F32)
        for q in range(PACK):
            nc.gpsimd.tensor_scalar(
                out=select[:, :, q, :],
                in0=ident_f32[:].rearrange("p (c t) -> p t c", t=PACK),
                scalar1=1.0,
                scalar2=0.0,
                op0=ALU.mult,
                op1=ALU.add,
            )
        quarter = keep.tile([P, PACK], F32)
        nc.vector.tensor_reduce(
            out=quarter[:], in_=ident_f32[:].rearrange("p (q c) -> p q c", q=PACK), axis=AXIS.X, op=ALU.add
        )
        bias = keep.tile([P, COUT], F32)

        ag_words = [keep.tile([P, 2, CHUNK], F32, name="ag_words%d" % c) for c in range(N_CHUNKS)]
        ag_rows = [keep.tile([P, PACK, CHUNK], BF16, name="ag_rows%d" % c) for c in range(N_CHUNKS)]

        def ag_values(c, g, t):
            if g == 0:
                return ag_words[c][:, t // 2, :].bitcast(BF16)[:, t % 2 :: 2]
            return ag_rows[c][:, t, :]

        w_codes = keep.tile([P, 2, PASSES, COUT], U32, align_bytes=64)
        w_scales = keep.tile([P, 2, PASSES, COUT], U8, align_bytes=64)
        stats = keep.tile([P, PACK, N_CHUNKS, BN_STATS_DIM], F32)
        mean_var = keep.tile([P, PACK, 2], F32)
        diagonal = keep.tile([P, PE_STAT_TILES, P], F32)
        squares_mean = keep.tile([P, PE_STAT_TILES], F32)
        row_sums = keep.tile([P, PACK, N_CHUNKS], F32)
        row_sum = keep.tile([P, PACK], F32)
        masked = keep.tile([P, PACK, PACK], F32)
        mean_of_squares = keep.tile([P, PACK], F32)
        mean_1 = keep.tile([P, PACK], F32)
        mean_squared = keep.tile([P, PACK], F32)
        var_1 = keep.tile([P, PACK], F32)
        mean = [mean_var[:, :, 0], mean_1[:]]
        std = [keep.tile([P, PACK], F32, name="std%d" % g) for g in range(PASSES)]
        inv_std = [keep.tile([P, PACK], F32, name="inv_std%d" % g) for g in range(PASSES)]
        bn_scale = [keep.tile([P, PACK], F32, name="bn_scale%d" % g) for g in range(PASSES)]
        scaled_mean = [keep.tile([P, PACK], F32, name="scaled_mean%d" % g) for g in range(PASSES)]
        bn_shift = [keep.tile([P, PACK], F32, name="bn_shift%d" % g) for g in range(PASSES)]

        sources = [ag_chunks[c] for c in range(N_CHUNKS)] + [feat_chunks[c] for c in range(N_CHUNKS)]
        loaded = []
        w_rows = []

        def load_next_chunk():
            if len(loaded) < len(sources):
                chunk = natural.tile([P, SUB, CHANNELS], BF16, tag="natural", name="chunk")
                if not loaded:
                    for g in range(PASSES):
                        channels = slice(g * K_PASS, (g + 1) * K_PASS)
                        for i0 in range(0, SUB, 2):
                            nc.sync.dma_start(
                                out=chunk[:, i0 : i0 + 2, channels], in_=sources[0][:, i0 : i0 + 2, channels]
                            )
                else:
                    nc.sync.dma_start(out=chunk[:], in_=sources[len(loaded)])
                loaded.append(chunk)

        def load_weight(weight):
            w_raw = feat_pool.tile([P, PASSES, PACK * COUT], BF16, align_bytes=64, bufs=4, tag="feat_grouped", name="w_raw")
            nc.sync.dma_start(out=w_raw[:], in_=weight.rearrange("(g p t) n -> p g (t n)", p=P, t=PACK))
            w_rows.append(w_raw[:].rearrange("p g (t n) -> p (g t) n", t=PACK))

        feat_grouped = {}
        feat_operands = {}
        h_normed = {}
        h_grouped = {}
        h_operands = {}
        products = {}

        def keep_clock_up(pool, count):
            unread = pool.tile([P, COUT], F32, tag="bank", name="unread")
            for k in range(count):
                nc.tensor.matmul(out=unread[:], lhsT=ones[:, 0:P], rhs=ones[:], start=True, stop=True)

        def transpose_feat(c):
            feat_words = loaded[N_CHUNKS + c][:].bitcast(F32)
            feat_grouped[c] = feat_pool.tile(
                [P, PASSES, CHUNK * PACK], BF16, align_bytes=64, bufs=4, tag="feat_grouped", name="grouped"
            )
            grouped_words = feat_grouped[c][:].bitcast(F32)
            for g in range(PASSES):
                for i0 in range(0, SUB, 2):
                    bank = turned.tile([P, 2, 2, P], F32, tag="bank")
                    for u in range(2):
                        for ii in range(2):
                            first = 2 * g * P
                            nc.tensor.transpose(
                                bank[:, u, ii, :],
                                feat_words[:, i0 + ii, first + u : first + 2 * P : 2],
                                ident_f32[:],
                            )
                    nc.scalar.copy(
                        out=grouped_words[:, g, i0 * P * 2 : (i0 + 2) * P * 2].rearrange("p (q u) -> p q u", u=2),
                        in_=bank[:].rearrange("p u i q -> p (i q) u"),
                    )
            load_next_chunk()

        def quantise_feat(c):
            feat_codes = feat_pool.tile([P, PASSES, CHUNK], U32, align_bytes=64)
            feat_scales = feat_pool.tile([P, PASSES, CHUNK], U8, align_bytes=64)
            nc.vector.quantize_mx(
                out=feat_codes[:].rearrange("p g q -> p (g q)").bitcast(FP8X4),
                scales=feat_scales[:].rearrange("p g q -> p (g q)"),
                in_=feat_grouped[c][:].rearrange("p g x -> p (g x)"),
            )
            feat_operands[c] = (feat_codes, feat_scales)

        def root(g, var):
            nc.scalar.activation(out=std[g][:], in_=var, func=ACT.Sqrt, bias=eps[:], scale=1.0)

        def scale_and_shift(g):
            nc.vector.reciprocal(out=inv_std[g][:], in_=std[g][:])
            nc.vector.tensor_mul(out=bn_scale[g][:], in0=gain_shift[:, 0, g, :], in1=inv_std[g][:])
            nc.vector.tensor_mul(out=scaled_mean[g][:], in0=mean[g], in1=bn_scale[g][:])
            nc.vector.tensor_sub(out=bn_shift[g][:], in0=gain_shift[:, 1, g, :], in1=scaled_mean[g][:])

        def batch_norm(c, g):
            h_normed[c, g] = h_pool.tile([P, PACK, CHUNK], BF16, bufs=4, name="h_normed")
            for t in range(PACK):
                nc.vector.tensor_scalar(
                    out=h_normed[c, g][:, t, :],
                    in0=ag_values(c, g, t),
                    scalar1=bn_scale[g][:, t : t + 1],
                    scalar2=bn_shift[g][:, t : t + 1],
                    op0=ALU.mult,
                    op1=ALU.add,
                )

        def relu_and_regroup(c, g):
            if c not in h_grouped:
                h_grouped[c] = h_pool.tile([P, PASSES, CHUNK, PACK], BF16, align_bytes=64, name="h_grouped")
            grouped = by_runs_dst(h_grouped[c][:, g, :, :])
            rows = by_runs_src(h_normed[c, g][:])
            if g == PASSES - 1 and c in VECTOR_REGROUPS:
                nc.vector.tensor_scalar_max(out=grouped, in0=rows, scalar1=0.0)
            else:
                nc.scalar.activation(out=grouped, in_=rows, func=ACT.Relu)

        def quantise_h(c):
            h_codes = h_pool.tile([P, PASSES, CHUNK], U32, align_bytes=64)
            h_scales = h_pool.tile([P, PASSES, CHUNK], U8, align_bytes=64)
            for g in range(PASSES):
                nc.vector.quantize_mx(
                    out=h_codes[:, g, :].bitcast(FP8X4),
                    scales=h_scales[:, g, :],
                    in_=h_grouped[c][:, g, :, :].rearrange("p q t -> p (q t)"),
                )
            h_operands[c] = (h_codes, h_scales)

        with ExitStack() as part1:
            w_stage = part1.enter_context(tc.tile_pool(name="w_stage", bufs=1))
            turned = part1.enter_context(tc.psum_pool(name="turned", bufs=AG_TURN_BANKS))
            sums_psum = part1.enter_context(tc.psum_pool(name="sums_psum", bufs=1))
            squares = [
                sums_psum.tile([P, SQUARE_COLUMNS], F32, name="squares%d" % q) for q in range(PE_STAT_TILES)
            ]
            blocks = N_CHUNKS * SUB

            for k in range(NATURAL_BUFS - 2):
                load_next_chunk()
            load_weight(W_feat)
            for k in range(2):
                load_next_chunk()
            load_weight(W_ag)
            w_grouped = w_stage.tile([P, 2, PASSES, COUT, PACK], BF16, align_bytes=64)

            def group_weight(w, g):
                nc.gpsimd.tensor_scalar(
                    out=w_grouped[:, w, g, :, :],
                    in0=w_rows[w][:, g * PACK : (g + 1) * PACK, :].rearrange("p t n -> p n t"),
                    scalar1=1.0,
                    scalar2=0.0,
                    op0=ALU.mult,
                    op1=ALU.add,
                )

            def quantise_weight(w):
                nc.vector.quantize_mx(
                    out=w_codes[:, w, :, :].rearrange("p g n -> p (g n)").bitcast(FP8X4),
                    scales=w_scales[:, w, :, :].rearrange("p g n -> p (g n)"),
                    in_=w_grouped[:, w, :, :, :].rearrange("p g n t -> p (g n t)"),
                )

            for w in range(2):
                for g in range(PASSES):
                    group_weight(w, g)

            keep_clock_up(turned, WARM_UP_MATMULS)
            for c in range(N_CHUNKS):
                ag_nat = loaded[c]
                nat_words = ag_nat[:].bitcast(F32)
                for g in range(PASSES):
                    for u in range(2):
                        bank = turned.tile([P, SUB, P], F32, tag="bank")
                        for i in range(SUB):
                            every_2nd = nat_words[:, i, 2 * g * P + u : 2 * (g + 1) * P : 2]
                            nc.tensor.transpose(bank[:, i, :], every_2nd, ident_f32[:])
                        turned_words = bank[:].rearrange("p i q -> p (i q)")
                        if g == 0:
                            nc.scalar.copy(out=ag_words[c][:, u, :], in_=turned_words)
                            if u == 1:
                                for t in range(PACK):
                                    nc.vector.bn_stats(out=stats[:, t, c, :], in_=ag_values(c, g, t))
                        else:
                            for e in range(2):
                                t = 2 * u + e
                                nc.scalar.activation(
                                    out=ag_rows[c][:, t, :],
                                    in_=turned_words.bitcast(BF16)[:, e::2],
                                    func=ACT.Copy,
                                    accum_out=row_sums[:, t, c : c + 1],
                                )
                    for q in (2 * g, 2 * g + 1):
                        for i in range(SUB):
                            end = K_PASS + (q + 1) * P
                            block = ag_nat[:, i, end - P : end]
                            b = c * SUB + i
                            nc.tensor.matmul(
                                out=squares[q][:],
                                lhsT=block,
                                rhs=ag_nat[:, i, end - SQUARE_COLUMNS : end],
                                start=(b == 0),
                                stop=(b == blocks - 1),
                            )
                if c == SMALL_VECTORS_CHUNK:
                    vector_cols = turned.tile([P, PACK, P], BF16, tag="bank")
                    for t in range(PACK):
                        nc.tensor.transpose(vector_cols[:, t, :], vector_rows[:, t::PACK], ident_bf16[:])
                    nc.scalar.copy(
                        out=gain_shift[:].rearrange("p v g t -> p (v g) t"),
                        in_=vector_cols[:, :, 0 : 2 * PASSES].rearrange("p t r -> p r t"),
                    )
                    bias_sum = turned.tile([P, COUT], F32, tag="bank")
                    nc.tensor.matmul(out=bias_sum[:], lhsT=ones[:, 0:P], rhs=bias_rows[:], start=True, stop=True)
                    nc.scalar.copy(out=bias[:], in_=bias_sum[:])
                if c in WEIGHT_CHUNKS:
                    quantise_weight(WEIGHT_CHUNKS.index(c))
                load_next_chunk()

            for t in range(PACK):
                nc.vector.bn_aggr(out=mean_var[:, t, :], in_=stats[:, t, :, :].rearrange("p c s -> p (c s)"))
            for q in range(PE_STAT_TILES):
                nc.vector.scalar_tensor_tensor(
                    out=diagonal[:, q, :],
                    in0=squares[q][:, SQUARE_COLUMNS - P : SQUARE_COLUMNS],
                    scalar=1.0 / POINTS,
                    in1=ident_f32[:],
                    op0=ALU.mult,
                    op1=ALU.mult,
                    accum_out=squares_mean[:, q : q + 1],
                )
            nc.vector.tensor_reduce(out=row_sum[:], in_=row_sums[:], axis=AXIS.X, op=ALU.add)

        result_pool = ctx.enter_context(tc.tile_pool(name="result_pool", bufs=8, reuse_waits="tile"))
        turned = ctx.enter_context(tc.psum_pool(name="feat_turned", bufs=FEAT_TURN_BANKS, reuse_waits="tile"))
        product_psum = ctx.enter_context(tc.psum_pool(name="product_psum", bufs=PRODUCT_BANKS, reuse_waits="tile"))

        root(0, mean_var[:, :, 1])
        transpose_feat(0)
        keep_clock_up(product_psum, 2)
        scale_and_shift(0)
        batch_norm(0, 0)
        relu_and_regroup(0, 0)
        moved = product_psum.tile([P, PACK, PACK], F32, tag="bank")
        for t in range(PACK):
            nc.tensor.matmul(
                out=moved[:, t, :],
                lhsT=select[:, t, :, :].rearrange("p q c -> p (q c)"),
                rhs=squares_mean[:],
                start=True,
                stop=True,
            )
        keep_clock_up(product_psum, 2)
        nc.vector.tensor_scalar_mul(out=mean_1[:], in0=row_sum[:], scalar1=1.0 / POINTS)
        nc.vector.tensor_tensor(
            out=masked[:], in0=moved[:], in1=quarter[:].unsqueeze(1).to_broadcast([P, PACK, PACK]), op=ALU.mult
        )
        nc.vector.tensor_mul(out=mean_squared[:], in0=mean_1[:], in1=mean_1[:])
        nc.vector.tensor_reduce(out=mean_of_squares[:], in_=masked[:], axis=AXIS.X, op=ALU.add)
        nc.vector.tensor_sub(out=var_1[:], in0=mean_of_squares[:], in1=mean_squared[:])
        nc.vector.tensor_scalar_max(out=var_1[:], in0=var_1[:], scalar1=0.0)
        root(1, var_1[:])
        transpose_feat(1)
        quantise_feat(0)
        scale_and_shift(1)
        batch_norm(0, 1)
        relu_and_regroup(0, 1)
        transpose_feat(2)
        quantise_h(0)
        for g in range(PASSES):
            batch_norm(1, g)

        def multiply(c):
            for i in range(SUB):
                points = slice(i * P, (i + 1) * P)
                product = product_psum.tile([P, COUT], F32, tag="bank", name="product")
                for w, (codes, scales) in enumerate((feat_operands[c], h_operands[c])):
                    for g in range(PASSES):
                        nc.tensor.matmul_mx(
                            out=product[:],
                            lhsT=codes[:, g, points].bitcast(FP8X4),
                            lhsT_scale=scales[:, g, points],
                            rhs=w_codes[:, w, g, :].bitcast(FP8X4),
                            rhs_scale=w_scales[:, w, g, :],
                            start=(w == 0 and g == 0),
                            stop=(w == 1 and g == PASSES - 1),
                        )
                products[c, i] = product

        def add_bias_and_store(c, sub_tiles):
            for i in sub_tiles:
                result = result_pool.tile([P, COUT], F32)
                nc.vector.tensor_tensor(out=result[:], in0=products[c, i][:], in1=bias[:], op=ALU.add)
                nc.sync.dma_start(out=out_chunks[c][:, i, :], in_=result[:])

        first_half = range(SUB // 2)
        second_half = range(SUB // 2, SUB)
        for c in range(N_CHUNKS):
            if c > 0:
                quantise_h(c)
                add_bias_and_store(c - 1, second_half)
            if c + FEAT_TURN_AHEAD < N_CHUNKS:
                transpose_feat(c + FEAT_TURN_AHEAD)
            multiply(c)
            if c + 2 < N_CHUNKS:
                for g in range(PASSES):
                    batch_norm(c + 2, g)
            if c + 1 < N_CHUNKS:
                quantise_feat(c + 1)
                for g in range(PASSES):
                    relu_and_regroup(c + 1, g)
            add_bias_and_store(c, first_half)
        add_bias_and_store(N_CHUNKS - 1, second_half)
